import numpy as np
import ml_dtypes


def mxq(x, axis, fmt="e4m3"):
    dtype, down = {"e4m3": (ml_dtypes.float8_e4m3fn, 7), "e5m2": (ml_dtypes.float8_e5m2, 14)}[fmt]
    v = np.moveaxis(np.asarray(x, np.float32).astype(ml_dtypes.bfloat16).astype(np.float64), axis, -1)
    blocks = v.reshape(v.shape[:-1] + (-1, 32))
    amax = np.abs(blocks).max(-1, keepdims=True)
    byte = np.maximum(np.where(amax > 0, np.frexp(amax)[1] - 1 + 127, 0) - down, 1)
    scale = np.exp2(byte - 127.0)
    codes = (blocks / scale).astype(np.float32).astype(dtype).astype(np.float64)
    return np.moveaxis((codes * scale).reshape(v.shape), -1, axis)


WIDE = False


def mx_kscale(k):
    if not WIDE:
        return np.ones(k)
    levels = np.array([10, -10, 5, -5, 0])
    a = np.random.permutation(np.resize(levels, k // 512 * 4)).reshape(k // 512, 4)
    idx = np.arange(k)
    return np.exp2(a[idx // 512, idx % 128 // 32])


BF16 = ml_dtypes.bfloat16


def bf(x):
    return np.asarray(x, np.float32).astype(BF16)


def f64(x):
    return np.asarray(x).astype(np.float64)


B, G, WS, C, NH, LK, BANK = 1, 64, 32, 512, 4, 384, 128
N = G * G
NW = WS * WS
NG = G // WS
BW = B * NG * NG
DH = C // NH


def setup_inputs():
    s = mx_kscale(C)
    return {"x": bf(np.random.standard_normal((B, N, C)) * s),
            "kv_w": bf(np.random.standard_normal((C, 2 * C)) / np.sqrt(C) / s[:, None]),
            "kv_b": bf(np.random.standard_normal(2 * C) * 0.3),
            "E_k": bf(np.random.standard_normal((NW, LK)) / np.sqrt(NW)),
            "E_v": bf(np.random.standard_normal((NW, LK)) * 2.0 / np.sqrt(NW))}


def reference(x, kv_w, kv_b, E_k, E_v):
    xw = f64(x).reshape(B, NG, WS, NG, WS, C).transpose(0, 1, 3, 2, 4, 5).reshape(BW, NW, C)
    kv = (mxq(xw, 2, "e4m3") @ mxq(f64(kv_w), 0, "e4m3")) + f64(kv_b)
    k, v = kv[..., :C], kv[..., C:]
    k_c = mxq(f64(E_k), 0, "e4m3").T @ mxq(k, 1, "e4m3")
    v_c = mxq(f64(E_v), 0, "e4m3").T @ mxq(v, 1, "e4m3")
    return (k_c.reshape(BW, LK, NH, DH).transpose(0, 2, 1, 3), v_c.reshape(BW, LK, NH, DH).transpose(0, 2, 1, 3))

@@ -1,0 +1,263 @@
+from contextlib import ExitStack
+
+import concourse.mybir as mybir
+from concourse.masks import make_identity
+
+F32 = mybir.dt.float32
+BF16 = mybir.dt.bfloat16
+U32 = mybir.dt.uint32
+U8 = mybir.dt.uint8
+FP8X4 = mybir.dt.float8_e4m3fn_x4
+
+P = 128
+PACK = 4
+CHANNELS = 512
+HALF = 512
+PIECE = 256
+BLOCK = 128
+LK = 384
+ROW_TILES = LK // P
+PASSES = 2
+E_TILES = 2 * PASSES * ROW_TILES
+BAND_ROWS = 16
+GROUPS = 8
+LAG = 2
+E_START = 6
+
+FLOPS = 2 * 4096 * 512 * 1024 + 2 * 2 * 4 * 384 * 1024 * 512
+
+
+def tile_efficientspatialwindowattention_pa_kernel(tc, x, kv_w, kv_b, E_k, E_v, out_0, out_1):
+    nc = tc.nc
+    outs = [out_0, out_1]
+    compressors = [E_k, E_v]
+    x_rows = x.rearrange("o (g p j) ch -> (o g) p (j ch)", p=P, j=PACK)
+
+    with ExitStack() as ctx:
+        keep = ctx.enter_context(tc.tile_pool(name="keep", bufs=1))
+        x_stage = ctx.enter_context(tc.tile_pool(name="x_stage", bufs=4))
+        kv_stage = ctx.enter_context(tc.tile_pool(name="kv_stage", bufs=3))
+        out_stage = ctx.enter_context(tc.tile_pool(name="out_stage", bufs=4))
+        turned_banks = ctx.enter_context(tc.psum_pool(name="turned_banks", bufs=2))
+        kv_banks = ctx.enter_context(tc.psum_pool(name="kv_banks", bufs=3))
+        out_banks = ctx.enter_context(tc.psum_pool(name="out_banks", bufs=3))
+        ctx.enter_context(tc.manual_schedule())
+
+        bands = [(c, wr) for c in range(PASSES) for wr in range(2)]
+        pieces = [
+            (c, wr, half, side, pair)
+            for (c, wr) in bands
+            for half in range(2)
+            for side in range(2)
+            for pair in range(2)
+        ]
+
+        identity = keep.tile([P, P], F32)
+        ones = keep.tile([P, P], BF16)
+        bias_row = keep.tile([P, 2 * HALF], BF16)
+        bias_all = keep.tile([P, 2 * HALF], F32)
+        w_raw = keep.tile([P, PACK, 2 * HALF], BF16)
+        w_grouped = keep.tile([P, 2 * HALF, PACK], BF16, align_bytes=64)
+        w_codes = keep.tile([P, 2 * HALF], U32, align_bytes=64)
+        w_scales = keep.tile([P, 2 * HALF], U8, align_bytes=64)
+        e_raw = keep.tile([P, 2, PASSES, PACK, LK], BF16)
+        e_grouped = keep.tile([P, E_TILES, P, PACK], BF16, align_bytes=64)
+        e_codes = keep.tile([P, E_TILES, P], U32, align_bytes=64)
+        e_scales = keep.tile([P, E_TILES, P], U8, align_bytes=64)
+        x_raw = {}
+        x_grouped = {}
+        x_codes = {}
+        x_scales = {}
+        for c, wr in bands:
+            x_raw[c, wr] = keep.tile([P, 2, PACK * CHANNELS], BF16, name="x_raw_%d%d" % (c, wr))
+            for side in range(2):
+                tail = "_%d%d%d" % (c, wr, side)
+                x_codes[c, wr, side] = keep.tile([P, PACK * P], U32, name="x_codes" + tail, align_bytes=64)
+                x_scales[c, wr, side] = keep.tile([P, PACK * P], U8, name="x_scales" + tail, align_bytes=64)
+        kv_grouped = {}
+        kv_codes = {}
+        kv_scales = {}
+        for piece in pieces:
+            tail = "_%d%d%d%d%d" % piece
+            kv_codes[piece] = keep.tile([P, PIECE], U32, name="kv_codes" + tail, align_bytes=64)
+            kv_scales[piece] = keep.tile([P, PIECE], U8, name="kv_scales" + tail, align_bytes=64)
+
+        def load_weights(half):
+            cols = slice(half * HALF, (half + 1) * HALF)
+            for u in range(2):
+                nc.sync.dma_start(
+                    out=w_raw[:, 2 * u : 2 * u + 2, cols],
+                    in_=kv_w[2 * P * u : 2 * P * (u + 1), cols].rearrange("(q e) n -> q e n", e=2),
+                )
+
+        def load_band(c, wr):
+            first = 2 * (2 * wr + c)
+            for a in range(2):
+                nc.sync.dma_start(out=x_raw[c, wr][:, a, :], in_=x_rows[first + a])
+
+        def load_compressor(half):
+            nc.sync.dma_start(
+                out=e_raw[:, half].rearrange("p c t l -> p c (t l)"),
+                in_=compressors[half].rearrange("(c p t) l -> p c (t l)", c=PASSES, t=PACK),
+            )
+
+        def group_weights(copy, half):
+            cols = slice(half * HALF, (half + 1) * HALF)
+            copy(
+                out=w_grouped[:, cols, :].rearrange("p (n i) t -> p n t i", i=4),
+                in_=w_raw[:, :, cols].rearrange("p t (n i) -> p n t i", i=4),
+            )
+
+        def quantise_weights(half):
+            cols = slice(half * HALF, (half + 1) * HALF)
+            nc.vector.quantize_mx(
+                out=w_codes[:, cols].bitcast(FP8X4),
+                scales=w_scales[:, cols],
+                in_=w_grouped[:, cols, :].rearrange("p n t -> p (n t)"),
+            )
+
+        def turn_tokens(c, wr, j):
+            if j == 0:
+                for side in range(2):
+                    x_grouped[c, wr, side] = x_stage.tile(
+                        [P, PACK * P * PACK], BF16, name="x_grouped", align_bytes=64
+                    )
+            turned = turned_banks.tile([P, 2, BAND_ROWS, 2, GROUPS], F32)
+            for u in range(2):
+                for a in range(2):
+                    words = x_raw[c, wr][:, a, :].bitcast(F32)
+                    first = (2 * j + u) * P
+                    nc.tensor.transpose(
+                        turned[:, u, 8 * a : 8 * a + 8, :, :].rearrange("p r s g -> p (r s g)"),
+                        words[:, first : first + P],
+                        identity[:],
+                    )
+            for side in range(2):
+                pairs = x_grouped[c, wr, side][:].bitcast(F32)
+                pairs = pairs.rearrange("p (j r g u) -> p j r g u", j=PACK, r=BAND_ROWS, g=GROUPS)
+                nc.scalar.copy(out=pairs[:, j], in_=turned[:, :, :, side, :].rearrange("p u r g -> p r g u"))
+
+        def quantise_tokens(c, wr):
+            for side in range(2):
+                nc.vector.quantize_mx(
+                    out=x_codes[c, wr, side][:].bitcast(FP8X4),
+                    scales=x_scales[c, wr, side][:],
+                    in_=x_grouped[c, wr, side][:],
+                )
+
+        def project(piece, block):
+            c, wr, half, side, pair = piece
+            first = half * HALF + pair * PIECE + block * BLOCK
+            cols = slice(first, first + BLOCK)
+            kv_bank = kv_banks.tile([P, PACK, BLOCK], F32)
+            for j in range(PACK):
+                tokens = slice(j * P, (j + 1) * P)
+                nc.tensor.matmul_mx(
+                    out=kv_bank[:, j, :],
+                    lhsT=x_codes[c, wr, side][:, tokens].bitcast(FP8X4),
+                    lhsT_scale=x_scales[c, wr, side][:, tokens],
+                    rhs=w_codes[:, cols].bitcast(FP8X4),
+                    rhs_scale=w_scales[:, cols],
+                    start=True,
+                    stop=True,
+                )
+            nc.vector.tensor_tensor(
+                out=kv_grouped[piece][:, block * BLOCK : (block + 1) * BLOCK, :],
+                in0=kv_bank[:].rearrange("p j n -> p n j"),
+                in1=bias_all[:, cols].unsqueeze(2).to_broadcast([P, BLOCK, PACK]),
+                op=mybir.AluOpType.add,
+            )
+
+        def quantise_piece(piece):
+            nc.vector.quantize_mx(
+                out=kv_codes[piece][:].bitcast(FP8X4),
+                scales=kv_scales[piece][:],
+                in_=kv_grouped[piece][:].rearrange("p n j -> p (n j)"),
+            )
+
+        def group_compressor(e):
+            half, c, m = e // (PASSES * ROW_TILES), (e // ROW_TILES) % PASSES, e % ROW_TILES
+            nc.scalar.copy(
+                out=e_grouped[:, e, :, :],
+                in_=e_raw[:, half, c, :, :].rearrange("p t (n m) -> p m n t", m=ROW_TILES)[:, m],
+            )
+
+        def quantise_compressor(tiles):
+            nc.vector.quantize_mx(
+                out=e_codes[:, tiles, :].rearrange("p e n -> p (e n)").bitcast(FP8X4),
+                scales=e_scales[:, tiles, :].rearrange("p e n -> p (e n)"),
+                in_=e_grouped[:, tiles, :, :].rearrange("p e n t -> p (e n t)"),
+            )
+
+        def compress(wr, half, side, pair):
+            result = out_stage.tile([P, 2, ROW_TILES, BLOCK], F32)
+            for m in range(ROW_TILES):
+                out_bank = out_banks.tile([P, 2, BLOCK], F32, tag="out_bank")
+                for c in range(PASSES):
+                    e = (half * PASSES + c) * ROW_TILES + m
+                    nc.tensor.matmul_mx(
+                        out=out_bank[:].rearrange("p h d -> p (h d)"),
+                        lhsT=e_codes[:, e, :].bitcast(FP8X4),
+                        lhsT_scale=e_scales[:, e, :],
+                        rhs=kv_codes[c, wr, half, side, pair][:].bitcast(FP8X4),
+                        rhs_scale=kv_scales[c, wr, half, side, pair][:],
+                        start=(c == 0),
+                        stop=(c == PASSES - 1),
+                    )
+                nc.scalar.copy(out=result[:, :, m, :], in_=out_bank[:])
+            heads = slice(2 * pair, 2 * pair + 2)
+            nc.sync.dma_start(
+                out=outs[half][2 * wr + side, heads].rearrange("h (n m) d -> n h (m d)", m=ROW_TILES),
+                in_=result[:].rearrange("p h m d -> p h (m d)"),
+            )
+
+        nc.vector.memset(bias_row[:], 0.0)
+        nc.vector.memset(ones[:], 1.0)
+        make_identity(nc, identity[:])
+        load_band(*bands[0])
+        nc.sync.dma_start(out=bias_row[0:1, :], in_=kv_b.unsqueeze(0))
+        load_weights(0)
+        load_weights(1)
+        load_band(*bands[1])
+        load_band(*bands[2])
+        load_compressor(0)
+        load_compressor(1)
+        load_band(*bands[3])
+
+        for half in range(2):
+            cols = slice(half * HALF, (half + 1) * HALF)
+            spread = out_banks.tile([P, HALF], F32, tag="out_bank")
+            nc.tensor.matmul(out=spread[:], lhsT=ones[:], rhs=bias_row[:, cols], start=True, stop=True)
+            nc.scalar.copy(out=bias_all[:, cols], in_=spread[:])
+
+        for j in range(PACK):
+            turn_tokens(*bands[0], j)
+        group_weights(nc.vector.tensor_copy, 0)
+        quantise_weights(0)
+        group_weights(nc.scalar.copy, 1)
+        quantise_tokens(*bands[0])
+
+        later_banks = [(c, wr, j) for (c, wr) in bands[1:] for j in range(PACK)]
+        first_value_piece = pieces.index((0, 0, 1, 0, 0))
+        for s, piece in enumerate(pieces):
+            for bank in later_banks[s : s + 1]:
+                turn_tokens(*bank)
+            if E_START <= s < E_START + E_TILES:
+                group_compressor(s - E_START)
+            kv_grouped[piece] = kv_stage.tile([P, PIECE, PACK], BF16, name="kv_grouped", align_bytes=64)
+            project(piece, 0)
+            if s >= 1:
+                quantise_piece(pieces[s - 1])
+            if s + LAG == first_value_piece:
+                quantise_weights(1)
+            project(piece, 1)
+            for c, wr, j in later_banks[s : s + 1]:
+                if j == PACK - 1:
+                    quantise_tokens(c, wr)
+            if E_START <= s < E_START + E_TILES and (s - E_START) % 4 == 3:
+                quantise_compressor(slice(s - E_START - 3, s - E_START + 1))
+            if s >= LAG and pieces[s - LAG][0] == PASSES - 1:
+                compress(*pieces[s - LAG][1:])
+        quantise_piece(pieces[-1])
+        for piece in pieces[-LAG:]:
+            compress(*piece[1:])

@@ -21,8 +21,13 @@ PASSES = 2
 E_TILES = 2 * PASSES * ROW_TILES
 BAND_ROWS = 16
 GROUPS = 8
-LAG = 2
-E_START = 6
+HEADS = 4
+TURNED = 3
+E_START = 1
+FIRST_OUT = 6
+OUT_RATE = 3
+TURNED_UNITS = range(1, 16)
+TILE_PLACE = [0, 1, 2]
 
 FLOPS = 2 * 4096 * 512 * 1024 + 2 * 2 * 4 * 384 * 1024 * 512
 
@@ -31,31 +36,29 @@ def tile_efficientspatialwindowattention_pa_kernel(tc, x, kv_w, kv_b, E_k, E_v, 
     nc = tc.nc
     outs = [out_0, out_1]
     compressors = [E_k, E_v]
-    x_rows = x.rearrange("o (g p j) ch -> (o g) p (j ch)", p=P, j=PACK)
+    x_parts = x.rearrange("o (b r w g j) ch -> (o b) w r g (j ch)", b=4, r=BAND_ROWS, w=2, g=GROUPS)
 
     with ExitStack() as ctx:
         keep = ctx.enter_context(tc.tile_pool(name="keep", bufs=1))
         x_stage = ctx.enter_context(tc.tile_pool(name="x_stage", bufs=4))
         kv_stage = ctx.enter_context(tc.tile_pool(name="kv_stage", bufs=3))
+        turned_stage = ctx.enter_context(tc.tile_pool(name="turned_stage", bufs=2))
         out_stage = ctx.enter_context(tc.tile_pool(name="out_stage", bufs=4))
         turned_banks = ctx.enter_context(tc.psum_pool(name="turned_banks", bufs=2))
+        channel_banks = ctx.enter_context(tc.psum_pool(name="channel_banks", bufs=1))
         kv_banks = ctx.enter_context(tc.psum_pool(name="kv_banks", bufs=3))
-        out_banks = ctx.enter_context(tc.psum_pool(name="out_banks", bufs=3))
+        out_banks = ctx.enter_context(tc.psum_pool(name="out_banks", bufs=2))
         ctx.enter_context(tc.manual_schedule())
 
-        bands = [(c, wr) for c in range(PASSES) for wr in range(2)]
-        pieces = [
-            (c, wr, half, side, pair)
-            for (c, wr) in bands
-            for half in range(2)
-            for side in range(2)
-            for pair in range(2)
-        ]
+        bands = [(c, wr) for wr in range(2) for c in range(PASSES)]
+        parts = [(c, wr, side) for (c, wr) in bands for side in range(2)]
+        units = [(c, wr, half, side) for (c, wr, side) in parts for half in range(2)]
 
         identity = keep.tile([P, P], F32)
         ones = keep.tile([P, P], BF16)
         bias_row = keep.tile([P, 2 * HALF], BF16)
         bias_all = keep.tile([P, 2 * HALF], F32)
+        bias_column = keep.tile([P, 2, 2], F32)
         w_raw = keep.tile([P, PACK, 2 * HALF], BF16)
         w_grouped = keep.tile([P, 2 * HALF, PACK], BF16, align_bytes=64)
         w_codes = keep.tile([P, 2 * HALF], U32, align_bytes=64)
@@ -68,19 +71,20 @@ def tile_efficientspatialwindowattention_pa_kernel(tc, x, kv_w, kv_b, E_k, E_v, 
         x_grouped = {}
         x_codes = {}
         x_scales = {}
-        for c, wr in bands:
-            x_raw[c, wr] = keep.tile([P, 2, PACK * CHANNELS], BF16, name="x_raw_%d%d" % (c, wr))
-            for side in range(2):
-                tail = "_%d%d%d" % (c, wr, side)
-                x_codes[c, wr, side] = keep.tile([P, PACK * P], U32, name="x_codes" + tail, align_bytes=64)
-                x_scales[c, wr, side] = keep.tile([P, PACK * P], U8, name="x_scales" + tail, align_bytes=64)
+        for part in parts:
+            tail = "_%d%d%d" % part
+            x_raw[part] = keep.tile([P, PACK * CHANNELS], BF16, name="x_raw" + tail)
+            x_codes[part] = keep.tile([P, PACK * P], U32, name="x_codes" + tail, align_bytes=64)
+            x_scales[part] = keep.tile([P, PACK * P], U8, name="x_scales" + tail, align_bytes=64)
         kv_grouped = {}
+        kv_turned = {}
+        results = {}
         kv_codes = {}
         kv_scales = {}
-        for piece in pieces:
-            tail = "_%d%d%d%d%d" % piece
-            kv_codes[piece] = keep.tile([P, PIECE], U32, name="kv_codes" + tail, align_bytes=64)
-            kv_scales[piece] = keep.tile([P, PIECE], U8, name="kv_scales" + tail, align_bytes=64)
+        for unit in units:
+            tail = "_%d%d%d%d" % unit
+            kv_codes[unit] = keep.tile([P, HALF], U32, name="kv_codes" + tail, align_bytes=64)
+            kv_scales[unit] = keep.tile([P, HALF], U8, name="kv_scales" + tail, align_bytes=64)
 
         def load_weights(half):
             cols = slice(half * HALF, (half + 1) * HALF)
@@ -90,10 +94,8 @@ def tile_efficientspatialwindowattention_pa_kernel(tc, x, kv_w, kv_b, E_k, E_v, 
                     in_=kv_w[2 * P * u : 2 * P * (u + 1), cols].rearrange("(q e) n -> q e n", e=2),
                 )
 
-        def load_band(c, wr):
-            first = 2 * (2 * wr + c)
-            for a in range(2):
-                nc.sync.dma_start(out=x_raw[c, wr][:, a, :], in_=x_rows[first + a])
+        def load_part(c, wr, side):
+            nc.sync.dma_start(out=x_raw[c, wr, side][:], in_=x_parts[2 * wr + c, side])
 
         def load_compressor(half):
             nc.sync.dma_start(
@@ -101,55 +103,45 @@ def tile_efficientspatialwindowattention_pa_kernel(tc, x, kv_w, kv_b, E_k, E_v, 
                 in_=compressors[half].rearrange("(c p t) l -> p c (t l)", c=PASSES, t=PACK),
             )
 
-        def group_weights(copy, half):
-            cols = slice(half * HALF, (half + 1) * HALF)
+        def group_weights(copy, first, width):
+            cols = slice(first, first + width)
             copy(
                 out=w_grouped[:, cols, :].rearrange("p (n i) t -> p n t i", i=4),
                 in_=w_raw[:, :, cols].rearrange("p t (n i) -> p n t i", i=4),
             )
 
-        def quantise_weights(half):
-            cols = slice(half * HALF, (half + 1) * HALF)
+        def quantise_weights(first, width):
+            cols = slice(first, first + width)
             nc.vector.quantize_mx(
                 out=w_codes[:, cols].bitcast(FP8X4),
                 scales=w_scales[:, cols],
                 in_=w_grouped[:, cols, :].rearrange("p n t -> p (n t)"),
             )
 
-        def turn_tokens(c, wr, j):
-            if j == 0:
-                for side in range(2):
-                    x_grouped[c, wr, side] = x_stage.tile(
-                        [P, PACK * P * PACK], BF16, name="x_grouped", align_bytes=64
-                    )
-            turned = turned_banks.tile([P, 2, BAND_ROWS, 2, GROUPS], F32)
-            for u in range(2):
-                for a in range(2):
-                    words = x_raw[c, wr][:, a, :].bitcast(F32)
-                    first = (2 * j + u) * P
-                    nc.tensor.transpose(
-                        turned[:, u, 8 * a : 8 * a + 8, :, :].rearrange("p r s g -> p (r s g)"),
-                        words[:, first : first + P],
-                        identity[:],
-                    )
-            for side in range(2):
-                pairs = x_grouped[c, wr, side][:].bitcast(F32)
-                pairs = pairs.rearrange("p (j r g u) -> p j r g u", j=PACK, r=BAND_ROWS, g=GROUPS)
-                nc.scalar.copy(out=pairs[:, j], in_=turned[:, :, :, side, :].rearrange("p u r g -> p r g u"))
+        def turn_tokens(part, pair):
+            if pair == 0:
+                x_grouped[part] = x_stage.tile([P, PACK * P * PACK], BF16, name="x_grouped", align_bytes=64)
+            turned = turned_banks.tile([P, 2, 2, P], F32, tag="turned")
+            words = x_raw[part][:].bitcast(F32)
+            for j in range(2):
+                for u in range(2):
+                    first = (2 * (2 * pair + j) + u) * P
+                    nc.tensor.transpose(turned[:, j, u, :], words[:, first : first + P], identity[:])
+            nc.scalar.copy(
+                out=x_grouped[part][:].bitcast(F32).rearrange("p (a j t u) -> p a j t u", a=2, j=2, u=2)[:, pair],
+                in_=turned[:].rearrange("p j u t -> p j t u"),
+            )
 
-        def quantise_tokens(c, wr):
-            for side in range(2):
-                nc.vector.quantize_mx(
-                    out=x_codes[c, wr, side][:].bitcast(FP8X4),
-                    scales=x_scales[c, wr, side][:],
-                    in_=x_grouped[c, wr, side][:],
-                )
+        def quantise_tokens(part):
+            nc.vector.quantize_mx(
+                out=x_codes[part][:].bitcast(FP8X4), scales=x_scales[part][:], in_=x_grouped[part][:]
+            )
 
-        def project(piece, block):
-            c, wr, half, side, pair = piece
-            first = half * HALF + pair * PIECE + block * BLOCK
+        def project(unit, block):
+            c, wr, half, side = unit
+            first = half * HALF + block * BLOCK
             cols = slice(first, first + BLOCK)
-            kv_bank = kv_banks.tile([P, PACK, BLOCK], F32)
+            kv_bank = kv_banks.tile([P, PACK, BLOCK], F32, tag="kv_bank")
             for j in range(PACK):
                 tokens = slice(j * P, (j + 1) * P)
                 nc.tensor.matmul_mx(
@@ -162,17 +154,55 @@ def tile_efficientspatialwindowattention_pa_kernel(tc, x, kv_w, kv_b, E_k, E_v, 
                     stop=True,
                 )
             nc.vector.tensor_tensor(
-                out=kv_grouped[piece][:, block * BLOCK : (block + 1) * BLOCK, :],
+                out=kv_grouped[unit][:, block * BLOCK : (block + 1) * BLOCK, :],
                 in0=kv_bank[:].rearrange("p j n -> p n j"),
                 in1=bias_all[:, cols].unsqueeze(2).to_broadcast([P, BLOCK, PACK]),
                 op=mybir.AluOpType.add,
             )
 
-        def quantise_piece(piece):
+        def project_turned(unit):
+            c, wr, half, side = unit
+            first = half * HALF + TURNED * BLOCK
+            cols = slice(first, first + BLOCK)
+            kv_bank = channel_banks.tile([P, 2, 2, P], F32)
+            nc.tensor.matmul_mx(
+                out=kv_bank[:].rearrange("n u e p -> n (u e p)"),
+                lhsT=w_codes[:, cols].bitcast(FP8X4),
+                lhsT_scale=w_scales[:, cols],
+                rhs=x_codes[c, wr, side][:].bitcast(FP8X4),
+                rhs_scale=x_scales[c, wr, side][:],
+                start=True,
+                stop=True,
+            )
+            kv_turned[unit] = turned_stage.tile([P, 2, P, 2], BF16, name="kv_turned")
+            nc.scalar.activation(
+                out=kv_turned[unit][:],
+                in_=kv_bank[:].rearrange("n u e p -> n u p e"),
+                func=mybir.ActivationFunctionType.Identity,
+                bias=bias_column[:, half, 0:1],
+            )
+
+        def turn_back(unit):
+            back = turned_banks.tile([P, 2, BLOCK], F32, tag="turned")
+            for u in range(2):
+                nc.tensor.transpose(
+                    back[:, u, :],
+                    kv_turned[unit][:, u].rearrange("n p e -> n (p e)").bitcast(F32),
+                    identity[:],
+                )
+            nc.scalar.copy(
+                out=kv_grouped[unit][:, TURNED * BLOCK :, :]
+                .rearrange("p n j -> p (n j)")
+                .bitcast(F32)
+                .rearrange("p (n u) -> p n u", u=2),
+                in_=back[:].rearrange("p u n -> p n u"),
+            )
+
+        def quantise_unit(unit, cols):
             nc.vector.quantize_mx(
-                out=kv_codes[piece][:].bitcast(FP8X4),
-                scales=kv_scales[piece][:],
-                in_=kv_grouped[piece][:].rearrange("p n j -> p (n j)"),
+                out=kv_codes[unit][:, cols].bitcast(FP8X4),
+                scales=kv_scales[unit][:, cols],
+                in_=kv_grouped[unit][:, cols, :].rearrange("p n j -> p (n j)"),
             )
 
         def group_compressor(e):
@@ -189,75 +219,120 @@ def tile_efficientspatialwindowattention_pa_kernel(tc, x, kv_w, kv_b, E_k, E_v, 
                 in_=e_grouped[:, tiles, :, :].rearrange("p e n t -> p (e n t)"),
             )
 
-        def compress(wr, half, side, pair):
-            result = out_stage.tile([P, 2, ROW_TILES, BLOCK], F32)
-            for m in range(ROW_TILES):
-                out_bank = out_banks.tile([P, 2, BLOCK], F32, tag="out_bank")
-                for c in range(PASSES):
-                    e = (half * PASSES + c) * ROW_TILES + m
-                    nc.tensor.matmul_mx(
-                        out=out_bank[:].rearrange("p h d -> p (h d)"),
-                        lhsT=e_codes[:, e, :].bitcast(FP8X4),
-                        lhsT_scale=e_scales[:, e, :],
-                        rhs=kv_codes[c, wr, half, side, pair][:].bitcast(FP8X4),
-                        rhs_scale=kv_scales[c, wr, half, side, pair][:],
-                        start=(c == 0),
-                        stop=(c == PASSES - 1),
-                    )
-                nc.scalar.copy(out=result[:, :, m, :], in_=out_bank[:])
-            heads = slice(2 * pair, 2 * pair + 2)
-            nc.sync.dma_start(
-                out=outs[half][2 * wr + side, heads].rearrange("h (n m) d -> n h (m d)", m=ROW_TILES),
-                in_=result[:].rearrange("p h m d -> p h (m d)"),
-            )
+        def compress(wr, half, side, first, heads, m, copy=nc.scalar.copy, banks=None):
+            key = (wr, half, side, first)
+            if m == 0:
+                results[key] = out_stage.tile([P, HEADS, ROW_TILES, BLOCK], F32, name="result")
+            cols = slice(first * BLOCK, (first + heads) * BLOCK)
+            if banks is None:
+                out_bank = out_banks.tile([P, HEADS, BLOCK], F32, tag="out_bank")
+            else:
+                out_bank = banks.tile([P, HEADS, BLOCK], F32, tag="kv_bank")
+            for c in range(PASSES):
+                e = (half * PASSES + c) * ROW_TILES + m
+                nc.tensor.matmul_mx(
+                    out=out_bank[:, 0:heads, :].rearrange("p h d -> p (h d)"),
+                    lhsT=e_codes[:, e, :].bitcast(FP8X4),
+                    lhsT_scale=e_scales[:, e, :],
+                    rhs=kv_codes[c, wr, half, side][:, cols].bitcast(FP8X4),
+                    rhs_scale=kv_scales[c, wr, half, side][:, cols],
+                    start=(c == 0),
+                    stop=(c == PASSES - 1),
+                )
+            copy(out=results[key][:, 0:heads, m, :], in_=out_bank[:, 0:heads, :])
+            if m == ROW_TILES - 1:
+                nc.sync.dma_start(
+                    out=outs[half][2 * wr + side, first : first + heads].rearrange("h (n m) d -> n h (m d)", m=ROW_TILES),
+                    in_=results[key][:, 0:heads].rearrange("p h m d -> p h (m d)"),
+                )
 
         nc.vector.memset(bias_row[:], 0.0)
         nc.vector.memset(ones[:], 1.0)
         make_identity(nc, identity[:])
-        load_band(*bands[0])
+        load_part(*parts[0])
         nc.sync.dma_start(out=bias_row[0:1, :], in_=kv_b.unsqueeze(0))
         load_weights(0)
         load_weights(1)
-        load_band(*bands[1])
-        load_band(*bands[2])
+        load_part(*parts[1])
+        load_part(*parts[2])
         load_compressor(0)
         load_compressor(1)
-        load_band(*bands[3])
+        for part in parts[3:]:
+            load_part(*part)
 
         for half in range(2):
             cols = slice(half * HALF, (half + 1) * HALF)
             spread = out_banks.tile([P, HALF], F32, tag="out_bank")
             nc.tensor.matmul(out=spread[:], lhsT=ones[:], rhs=bias_row[:, cols], start=True, stop=True)
             nc.scalar.copy(out=bias_all[:, cols], in_=spread[:])
+        column = out_banks.tile([P, 2, 2], F32, tag="out_bank")
+        for half in range(2):
+            first = half * HALF + TURNED * BLOCK
+            nc.tensor.matmul(
+                out=column[:, half, :], lhsT=bias_row[:, first : first + BLOCK], rhs=ones[:, 0:2], start=True, stop=True
+            )
+        nc.scalar.copy(out=bias_column[:], in_=column[:])
 
-        for j in range(PACK):
-            turn_tokens(*bands[0], j)
-        group_weights(nc.vector.tensor_copy, 0)
-        quantise_weights(0)
-        group_weights(nc.scalar.copy, 1)
-        quantise_tokens(*bands[0])
+        for pair in range(2):
+            turn_tokens(parts[0], pair)
+        group_weights(nc.vector.tensor_copy, 0, PIECE)
+        group_weights(nc.scalar.copy, PIECE, PIECE)
+        quantise_weights(0, PIECE)
+        quantise_tokens(parts[0])
 
-        later_banks = [(c, wr, j) for (c, wr) in bands[1:] for j in range(PACK)]
-        first_value_piece = pieces.index((0, 0, 1, 0, 0))
-        for s, piece in enumerate(pieces):
-            for bank in later_banks[s : s + 1]:
-                turn_tokens(*bank)
-            if E_START <= s < E_START + E_TILES:
-                group_compressor(s - E_START)
-            kv_grouped[piece] = kv_stage.tile([P, PIECE, PACK], BF16, name="kv_grouped", align_bytes=64)
-            project(piece, 0)
-            if s >= 1:
-                quantise_piece(pieces[s - 1])
-            if s + LAG == first_value_piece:
-                quantise_weights(1)
-            project(piece, 1)
-            for c, wr, j in later_banks[s : s + 1]:
-                if j == PACK - 1:
-                    quantise_tokens(c, wr)
-            if E_START <= s < E_START + E_TILES and (s - E_START) % 4 == 3:
-                quantise_compressor(slice(s - E_START - 3, s - E_START + 1))
-            if s >= LAG and pieces[s - LAG][0] == PASSES - 1:
-                compress(*pieces[s - LAG][1:])
-        quantise_piece(pieces[-1])
-        for piece in pieces[-LAG:]:
-            compress(*piece[1:])
+        whole = slice(0, HALF)
+        later_banks = [(part, pair) for part in parts[1:] for pair in range(2)]
+        first_windows = [(0, half, side, 0, HEADS, m) for side in range(2) for half in range(2) for m in range(ROW_TILES)]
+
+        def new_grouped(unit):
+            kv_grouped[unit] = kv_stage.tile([P, HALF, PACK], BF16, name="kv_grouped", align_bytes=64)
+
+        new_grouped(units[0])
+        for s, unit in enumerate(units):
+            here_turned = s in TURNED_UNITS
+            next_turned = s + 1 in TURNED_UNITS
+            blocks = range(TURNED) if here_turned else range(HEADS)
+            if s + 1 < len(units):
+                new_grouped(units[s + 1])
+            if s >= len(units) - 2:
+                tiles = [(1, *units[s - 2][2:], 0, HEADS, m) for m in range(ROW_TILES)]
+            else:
+                tiles = first_windows[max(0, OUT_RATE * (s - FIRST_OUT) // 2) : max(0, OUT_RATE * (s - FIRST_OUT + 1) // 2)]
+            banks = later_banks[0:2] if s == 0 else later_banks[s + 1 : s + 2]
+            for b in blocks:
+                project(unit, b)
+                if b == 0 and s >= 1:
+                    quantise_unit(units[s - 1], whole)
+                if b == 0 and s == 0:
+                    quantise_weights(PIECE, PIECE)
+                    group_weights(nc.scalar.copy, HALF, HALF)
+                if b == 2 and s == 0:
+                    quantise_weights(HALF, HALF)
+                if b == 1:
+                    if E_START <= s < E_START + E_TILES // 2:
+                        e = 2 * (s - E_START)
+                        group_compressor(e)
+                        group_compressor(e + 1)
+                        if e % 4 == 2:
+                            quantise_compressor(slice(e - 2, e + 2))
+                    for bank in banks:
+                        turn_tokens(*bank)
+                    if here_turned:
+                        turn_back(unit)
+                for i, tile in enumerate(tiles):
+                    if TILE_PLACE[i] == b:
+                        compress(*tile)
+                if b == 2 and s == len(units) - 1:
+                    quantise_unit(unit, slice(0, PIECE))
+                if b == blocks[-1] and next_turned:
+                    project_turned(units[s + 1])
+            for part, pair in banks:
+                if pair == 1:
+                    quantise_tokens(part)
+        last = units[-1]
+        quantise_unit(last, slice(PIECE, HALF))
+        for m in range(ROW_TILES):
+            compress(1, *units[-2][2:], 0, HEADS, m)
+        for pair in range(2):
+            for m in range(ROW_TILES):
+                compress(1, *last[2:], 2 * pair, 2, m, nc.vector.tensor_copy, kv_banks)

@@ -22,12 +22,16 @@ E_TILES = 2 * PASSES * ROW_TILES
 BAND_ROWS = 16
 GROUPS = 8
 HEADS = 4
+E_START = 0
 TURNED = 3
-E_START = 1
-FIRST_OUT = 6
-OUT_RATE = 3
-TURNED_UNITS = range(1, 16)
-TILE_PLACE = [0, 1, 2]
+TM = 2
+TURNED_UNITS = range(2, 16)
+WG = [(0, 0), (0, 1), (0, 2), (0, 3)]
+TILE0 = 9
+QP1 = (0, 2)
+QW1 = (1, 1)
+XB = 1
+EB = 1
 
 FLOPS = 2 * 4096 * 512 * 1024 + 2 * 2 * 4 * 384 * 1024 * 512
 
@@ -41,24 +45,22 @@ def tile_efficientspatialwindowattention_pa_kernel(tc, x, kv_w, kv_b, E_k, E_v, 
     with ExitStack() as ctx:
         keep = ctx.enter_context(tc.tile_pool(name="keep", bufs=1))
         x_stage = ctx.enter_context(tc.tile_pool(name="x_stage", bufs=4))
-        kv_stage = ctx.enter_context(tc.tile_pool(name="kv_stage", bufs=3))
+        kv_stage = ctx.enter_context(tc.tile_pool(name="kv_stage", bufs=2))
         turned_stage = ctx.enter_context(tc.tile_pool(name="turned_stage", bufs=2))
         out_stage = ctx.enter_context(tc.tile_pool(name="out_stage", bufs=4))
         turned_banks = ctx.enter_context(tc.psum_pool(name="turned_banks", bufs=2))
-        channel_banks = ctx.enter_context(tc.psum_pool(name="channel_banks", bufs=1))
-        kv_banks = ctx.enter_context(tc.psum_pool(name="kv_banks", bufs=3))
+        kv_banks = ctx.enter_context(tc.psum_pool(name="kv_banks", bufs=4))
         out_banks = ctx.enter_context(tc.psum_pool(name="out_banks", bufs=2))
         ctx.enter_context(tc.manual_schedule())
 
-        bands = [(c, wr) for wr in range(2) for c in range(PASSES)]
-        parts = [(c, wr, side) for (c, wr) in bands for side in range(2)]
-        units = [(c, wr, half, side) for (c, wr, side) in parts for half in range(2)]
+        parts = [(c, wr, side) for wr in range(2) for side in range(2) for c in range(PASSES)]
+        units = [(c, wr, half, side) for wr in range(2) for side in range(2) for half in range(2) for c in range(PASSES)]
 
         identity = keep.tile([P, P], F32)
         ones = keep.tile([P, P], BF16)
         bias_row = keep.tile([P, 2 * HALF], BF16)
         bias_all = keep.tile([P, 2 * HALF], F32)
-        bias_column = keep.tile([P, 2, 2], F32)
+        bias_column = keep.tile([P, 2, HEADS, 2], F32)
         w_raw = keep.tile([P, PACK, 2 * HALF], BF16)
         w_grouped = keep.tile([P, 2 * HALF, PACK], BF16, align_bytes=64)
         w_codes = keep.tile([P, 2 * HALF], U32, align_bytes=64)
@@ -86,8 +88,8 @@ def tile_efficientspatialwindowattention_pa_kernel(tc, x, kv_w, kv_b, E_k, E_v, 
             kv_codes[unit] = keep.tile([P, HALF], U32, name="kv_codes" + tail, align_bytes=64)
             kv_scales[unit] = keep.tile([P, HALF], U8, name="kv_scales" + tail, align_bytes=64)
 
-        def load_weights(half):
-            cols = slice(half * HALF, (half + 1) * HALF)
+        def load_weights(first, width):
+            cols = slice(first, first + width)
             for u in range(2):
                 nc.sync.dma_start(
                     out=w_raw[:, 2 * u : 2 * u + 2, cols],
@@ -96,6 +98,10 @@ def tile_efficientspatialwindowattention_pa_kernel(tc, x, kv_w, kv_b, E_k, E_v, 
 
         def load_part(c, wr, side):
             nc.sync.dma_start(out=x_raw[c, wr, side][:], in_=x_parts[2 * wr + c, side])
+
+        def load_half_part(c, wr, side, pair):
+            tokens = slice(2 * pair * CHANNELS, 2 * (pair + 1) * CHANNELS)
+            nc.sync.dma_start(out=x_raw[c, wr, side][:, tokens], in_=x_parts[2 * wr + c, side][:, :, tokens])
 
         def load_compressor(half):
             nc.sync.dma_start(
@@ -132,16 +138,18 @@ def tile_efficientspatialwindowattention_pa_kernel(tc, x, kv_w, kv_b, E_k, E_v, 
                 in_=turned[:].rearrange("p j u t -> p j t u"),
             )
 
-        def quantise_tokens(part):
+        def quantise_tokens(part, pairs=(0, 2)):
+            words = slice(2 * P * pairs[0], 2 * P * pairs[1])
+            values = slice(PACK * 2 * P * pairs[0], PACK * 2 * P * pairs[1])
             nc.vector.quantize_mx(
-                out=x_codes[part][:].bitcast(FP8X4), scales=x_scales[part][:], in_=x_grouped[part][:]
+                out=x_codes[part][:, words].bitcast(FP8X4), scales=x_scales[part][:, words], in_=x_grouped[part][:, values]
             )
 
-        def project(unit, block):
+        def multiply_tokens(unit, head):
             c, wr, half, side = unit
-            first = half * HALF + block * BLOCK
+            first = half * HALF + head * BLOCK
             cols = slice(first, first + BLOCK)
-            kv_bank = kv_banks.tile([P, PACK, BLOCK], F32, tag="kv_bank")
+            kv_bank = kv_banks.tile([P, PACK, BLOCK], F32, name="kv_bank")
             for j in range(PACK):
                 tokens = slice(j * P, (j + 1) * P)
                 nc.tensor.matmul_mx(
@@ -153,6 +161,12 @@ def tile_efficientspatialwindowattention_pa_kernel(tc, x, kv_w, kv_b, E_k, E_v, 
                     start=True,
                     stop=True,
                 )
+            return kv_bank
+
+        def project(unit, block):
+            first = unit[2] * HALF + block * BLOCK
+            cols = slice(first, first + BLOCK)
+            kv_bank = multiply_tokens(unit, block)
             nc.vector.tensor_tensor(
                 out=kv_grouped[unit][:, block * BLOCK : (block + 1) * BLOCK, :],
                 in0=kv_bank[:].rearrange("p j n -> p n j"),
@@ -160,11 +174,11 @@ def tile_efficientspatialwindowattention_pa_kernel(tc, x, kv_w, kv_b, E_k, E_v, 
                 op=mybir.AluOpType.add,
             )
 
-        def project_turned(unit):
+        def project_turned(unit, head):
             c, wr, half, side = unit
-            first = half * HALF + TURNED * BLOCK
+            first = half * HALF + head * BLOCK
             cols = slice(first, first + BLOCK)
-            kv_bank = channel_banks.tile([P, 2, 2, P], F32)
+            kv_bank = kv_banks.tile([P, 2, 2, P], F32, name="kv_bank")
             nc.tensor.matmul_mx(
                 out=kv_bank[:].rearrange("n u e p -> n (u e p)"),
                 lhsT=w_codes[:, cols].bitcast(FP8X4),
@@ -174,28 +188,30 @@ def tile_efficientspatialwindowattention_pa_kernel(tc, x, kv_w, kv_b, E_k, E_v, 
                 start=True,
                 stop=True,
             )
-            kv_turned[unit] = turned_stage.tile([P, 2, P, 2], BF16, name="kv_turned")
+            kv_turned[unit, head] = turned_stage.tile([P, 2, P, 2], BF16, name="kv_turned")
             nc.scalar.activation(
-                out=kv_turned[unit][:],
+                out=kv_turned[unit, head][:],
                 in_=kv_bank[:].rearrange("n u e p -> n u p e"),
                 func=mybir.ActivationFunctionType.Identity,
-                bias=bias_column[:, half, 0:1],
+                bias=bias_column[:, half, head, 0:1],
             )
 
-        def turn_back(unit):
-            back = turned_banks.tile([P, 2, BLOCK], F32, tag="turned")
-            for u in range(2):
-                nc.tensor.transpose(
-                    back[:, u, :],
-                    kv_turned[unit][:, u].rearrange("n p e -> n (p e)").bitcast(F32),
-                    identity[:],
-                )
+        def turn_back(unit, heads):
+            back = turned_banks.tile([P, 2, 2, BLOCK], F32, tag="turned")
+            count = len(heads)
+            for h, head in enumerate(heads):
+                for u in range(2):
+                    nc.tensor.transpose(
+                        back[:, h, u, :],
+                        kv_turned[unit, head][:, u].rearrange("n p e -> n (p e)").bitcast(F32),
+                        identity[:],
+                    )
             nc.scalar.copy(
-                out=kv_grouped[unit][:, TURNED * BLOCK :, :]
+                out=kv_grouped[unit][:, heads[0] * BLOCK : (heads[0] + count) * BLOCK, :]
                 .rearrange("p n j -> p (n j)")
                 .bitcast(F32)
-                .rearrange("p (n u) -> p n u", u=2),
-                in_=back[:].rearrange("p u n -> p n u"),
+                .rearrange("p (h n u) -> p h n u", h=count, u=2),
+                in_=back[:, 0:count].rearrange("p h u n -> p h n u"),
             )
 
         def quantise_unit(unit, cols):
@@ -205,18 +221,33 @@ def tile_efficientspatialwindowattention_pa_kernel(tc, x, kv_w, kv_b, E_k, E_v, 
                 in_=kv_grouped[unit][:, cols, :].rearrange("p n j -> p (n j)"),
             )
 
-        def group_compressor(e):
-            half, c, m = e // (PASSES * ROW_TILES), (e // ROW_TILES) % PASSES, e % ROW_TILES
-            nc.scalar.copy(
-                out=e_grouped[:, e, :, :],
-                in_=e_raw[:, half, c, :, :].rearrange("p t (n m) -> p m n t", m=ROW_TILES)[:, m],
-            )
+        def group_compressor(half, m):
+            for c in range(PASSES):
+                nc.scalar.copy(
+                    out=e_grouped[:, (half * ROW_TILES + m) * PASSES + c, :, :],
+                    in_=e_raw[:, half, c, :, :].rearrange("p t (n m) -> p m n t", m=ROW_TILES)[:, m],
+                )
 
-        def quantise_compressor(tiles):
+        def quantise_compressor(half, m):
+            first = (half * ROW_TILES + m) * PASSES
+            tiles = slice(first, first + PASSES)
             nc.vector.quantize_mx(
                 out=e_codes[:, tiles, :].rearrange("p e n -> p (e n)").bitcast(FP8X4),
                 scales=e_scales[:, tiles, :].rearrange("p e n -> p (e n)"),
                 in_=e_grouped[:, tiles, :, :].rearrange("p e n t -> p (e n t)"),
+            )
+
+        def compress_pass(out_bank, wr, half, side, first, heads, m, c):
+            e = (half * ROW_TILES + m) * PASSES + c
+            cols = slice(first * BLOCK, (first + heads) * BLOCK)
+            nc.tensor.matmul_mx(
+                out=out_bank[:, 0:heads, :].rearrange("p h d -> p (h d)"),
+                lhsT=e_codes[:, e, :].bitcast(FP8X4),
+                lhsT_scale=e_scales[:, e, :],
+                rhs=kv_codes[c, wr, half, side][:, cols].bitcast(FP8X4),
+                rhs_scale=kv_scales[c, wr, half, side][:, cols],
+                start=(c == 0),
+                stop=(c == PASSES - 1),
             )
 
         def compress(wr, half, side, first, heads, m, copy=nc.scalar.copy, banks=None):
@@ -227,18 +258,9 @@ def tile_efficientspatialwindowattention_pa_kernel(tc, x, kv_w, kv_b, E_k, E_v, 
             if banks is None:
                 out_bank = out_banks.tile([P, HEADS, BLOCK], F32, tag="out_bank")
             else:
-                out_bank = banks.tile([P, HEADS, BLOCK], F32, tag="kv_bank")
+                out_bank = banks[0].tile([P, HEADS, BLOCK], F32, tag=banks[1])
             for c in range(PASSES):
-                e = (half * PASSES + c) * ROW_TILES + m
-                nc.tensor.matmul_mx(
-                    out=out_bank[:, 0:heads, :].rearrange("p h d -> p (h d)"),
-                    lhsT=e_codes[:, e, :].bitcast(FP8X4),
-                    lhsT_scale=e_scales[:, e, :],
-                    rhs=kv_codes[c, wr, half, side][:, cols].bitcast(FP8X4),
-                    rhs_scale=kv_scales[c, wr, half, side][:, cols],
-                    start=(c == 0),
-                    stop=(c == PASSES - 1),
-                )
+                compress_pass(out_bank, wr, half, side, first, heads, m, c)
             copy(out=results[key][:, 0:heads, m, :], in_=out_bank[:, 0:heads, :])
             if m == ROW_TILES - 1:
                 nc.sync.dma_start(
@@ -249,90 +271,117 @@ def tile_efficientspatialwindowattention_pa_kernel(tc, x, kv_w, kv_b, E_k, E_v, 
         nc.vector.memset(bias_row[:], 0.0)
         nc.vector.memset(ones[:], 1.0)
         make_identity(nc, identity[:])
-        load_part(*parts[0])
+        for pair in range(2):
+            load_half_part(*parts[0], pair)
         nc.sync.dma_start(out=bias_row[0:1, :], in_=kv_b.unsqueeze(0))
-        load_weights(0)
-        load_weights(1)
+        load_weights(0, PIECE)
+        load_weights(PIECE, PIECE)
         load_part(*parts[1])
-        load_part(*parts[2])
+        load_weights(HALF, HALF)
         load_compressor(0)
+        load_part(*parts[2])
+        load_part(*parts[3])
         load_compressor(1)
-        for part in parts[3:]:
+        for part in parts[4:]:
             load_part(*part)
 
+        for pair in range(2):
+            turn_tokens(parts[0], pair)
         for half in range(2):
             cols = slice(half * HALF, (half + 1) * HALF)
             spread = out_banks.tile([P, HALF], F32, tag="out_bank")
             nc.tensor.matmul(out=spread[:], lhsT=ones[:], rhs=bias_row[:, cols], start=True, stop=True)
             nc.scalar.copy(out=bias_all[:, cols], in_=spread[:])
-        column = out_banks.tile([P, 2, 2], F32, tag="out_bank")
+        column = out_banks.tile([P, 2, HEADS, 2], F32, tag="out_bank")
         for half in range(2):
-            first = half * HALF + TURNED * BLOCK
-            nc.tensor.matmul(
-                out=column[:, half, :], lhsT=bias_row[:, first : first + BLOCK], rhs=ones[:, 0:2], start=True, stop=True
-            )
-        nc.scalar.copy(out=bias_column[:], in_=column[:])
+            for head in range(TURNED, HEADS):
+                first = half * HALF + head * BLOCK
+                nc.tensor.matmul(
+                    out=column[:, half, head, :], lhsT=bias_row[:, first : first + BLOCK], rhs=ones[:, 0:2], start=True, stop=True
+                )
+        nc.scalar.copy(out=bias_column[:, :, TURNED:HEADS], in_=column[:, :, TURNED:HEADS])
 
-        for pair in range(2):
-            turn_tokens(parts[0], pair)
         group_weights(nc.vector.tensor_copy, 0, PIECE)
         group_weights(nc.scalar.copy, PIECE, PIECE)
         quantise_weights(0, PIECE)
-        quantise_tokens(parts[0])
+        quantise_tokens(parts[0], (0, 1))
+        quantise_tokens(parts[0], (1, 2))
 
         whole = slice(0, HALF)
+        WE = [nc.vector.tensor_copy] * 4
         later_banks = [(part, pair) for part in parts[1:] for pair in range(2)]
-        first_windows = [(0, half, side, 0, HEADS, m) for side in range(2) for half in range(2) for m in range(ROW_TILES)]
+        bank_unit = [0, 0] + [max(1, j // 2) if j < 4 else j - 1 for j in range(2 * len(parts) - 4)]
+        slots = {}
+        groups = [(wr, half, side) for wr in range(2) for side in range(2) for half in range(2)]
+        tiles = [(*group, 0, HEADS, m) for group in groups[:-1] for m in range(ROW_TILES)]
+        for i, tile in enumerate(tiles):
+            slots.setdefault(min(3 * len(units) - 1, TILE0 + 2 * i), []).append(tile)
+        e_pairs = [(half, m) for half in range(2) for m in range(ROW_TILES)]
 
         def new_grouped(unit):
             kv_grouped[unit] = kv_stage.tile([P, HALF, PACK], BF16, name="kv_grouped", align_bytes=64)
 
+        KV = (kv_banks, "kv_bank")
+        TU = (turned_banks, "turned")
+        A, V = nc.scalar.copy, nc.vector.tensor_copy
+        ENG = [A, A, A, V, A, V]
         new_grouped(units[0])
         for s, unit in enumerate(units):
-            here_turned = s in TURNED_UNITS
-            next_turned = s + 1 in TURNED_UNITS
-            blocks = range(TURNED) if here_turned else range(HEADS)
-            if s + 1 < len(units):
-                new_grouped(units[s + 1])
-            if s >= len(units) - 2:
-                tiles = [(1, *units[s - 2][2:], 0, HEADS, m) for m in range(ROW_TILES)]
-            else:
-                tiles = first_windows[max(0, OUT_RATE * (s - FIRST_OUT) // 2) : max(0, OUT_RATE * (s - FIRST_OUT + 1) // 2)]
-            banks = later_banks[0:2] if s == 0 else later_banks[s + 1 : s + 2]
+            blocks = range(TURNED if s in TURNED_UNITS else HEADS)
+            banks = [k for k, u in zip(later_banks, bank_unit) if u == s]
+            ready = [k[0] for k, u in zip(later_banks, bank_unit) if u == s - 1 and k[1] == 1 and k[0] != parts[1]]
             for b in blocks:
                 project(unit, b)
-                if b == 0 and s >= 1:
-                    quantise_unit(units[s - 1], whole)
-                if b == 0 and s == 0:
-                    quantise_weights(PIECE, PIECE)
-                    group_weights(nc.scalar.copy, HALF, HALF)
-                if b == 2 and s == 0:
-                    quantise_weights(HALF, HALF)
-                if b == 1:
-                    if E_START <= s < E_START + E_TILES // 2:
-                        e = 2 * (s - E_START)
-                        group_compressor(e)
-                        group_compressor(e + 1)
-                        if e % 4 == 2:
-                            quantise_compressor(slice(e - 2, e + 2))
+                if b == 0:
+                    if 0 <= s - 1 - E_START < len(e_pairs):
+                        quantise_compressor(*e_pairs[s - 1 - E_START])
+                    if s == 0:
+                        quantise_weights(PIECE, PIECE)
+                    for part in ready:
+                        quantise_tokens(part)
+                    if 1 <= s < len(units) - 1:
+                        quantise_unit(units[s - 1], whole)
+                if b == 0:
+                    if s + 1 < len(units):
+                        new_grouped(units[s + 1])
+                for k in range(4):
+                    if (s, b) == WG[k]:
+                        group_weights(WE[k], HALF + k * BLOCK, BLOCK)
+                if b == XB:
                     for bank in banks:
                         turn_tokens(*bank)
-                    if here_turned:
-                        turn_back(unit)
-                for i, tile in enumerate(tiles):
-                    if TILE_PLACE[i] == b:
+                    if s in TURNED_UNITS:
+                        turn_back(unit, [TURNED])
+                if b == TM and s + 1 in TURNED_UNITS:
+                    project_turned(units[s + 1], TURNED)
+                if b == EB and 0 <= s - E_START < len(e_pairs):
+                    group_compressor(*e_pairs[s - E_START])
+                if (s, b) == QP1:
+                    quantise_tokens(parts[1])
+                if (s, b) == QW1:
+                    quantise_weights(HALF, HALF)
+                if b < 3:
+                    for tile in slots.get(3 * s + b, []):
                         compress(*tile)
-                if b == 2 and s == len(units) - 1:
+                if b == 1 and s == len(units) - 1:
+                    quantise_unit(units[s - 1], whole)
                     quantise_unit(unit, slice(0, PIECE))
-                if b == blocks[-1] and next_turned:
-                    project_turned(units[s + 1])
-            for part, pair in banks:
-                if pair == 1:
-                    quantise_tokens(part)
         last = units[-1]
         quantise_unit(last, slice(PIECE, HALF))
-        for m in range(ROW_TILES):
-            compress(1, *units[-2][2:], 0, HEADS, m)
+        wr, side, half = groups[-1][0], groups[-1][2], groups[-1][1]
+        last_banks = [TU, TU, KV, KV, KV, KV]
+        open_banks = {}
+        for k in range(2 * ROW_TILES):
+            pool, tag = last_banks[k]
+            open_banks[k] = pool.tile([P, HEADS, BLOCK], F32, name="open_bank", tag=tag)
+            compress_pass(open_banks[k], wr, half, side, 2 * (k // ROW_TILES), 2, k % ROW_TILES, 0)
         for pair in range(2):
+            result = out_stage.tile([P, HEADS, ROW_TILES, BLOCK], F32, name="result")
             for m in range(ROW_TILES):
-                compress(1, *last[2:], 2 * pair, 2, m, nc.vector.tensor_copy, kv_banks)
+                k = ROW_TILES * pair + m
+                compress_pass(open_banks[k], wr, half, side, 2 * pair, 2, m, 1)
+                ENG[k](out=result[:, 0:2, m, :], in_=open_banks[k][:, 0:2, :])
+            nc.sync.dma_start(
+                out=outs[half][2 * wr + side, 2 * pair : 2 * pair + 2].rearrange("h (n m) d -> n h (m d)", m=ROW_TILES),
+                in_=result[:, 0:2].rearrange("p h m d -> p h (m d)"),
+            )

@@ -99,10 +99,6 @@ def tile_efficientspatialwindowattention_pa_kernel(tc, x, kv_w, kv_b, E_k, E_v, 
         def load_part(c, wr, side):
             nc.sync.dma_start(out=x_raw[c, wr, side][:], in_=x_parts[2 * wr + c, side])
 
-        def load_half_part(c, wr, side, pair):
-            tokens = slice(2 * pair * CHANNELS, 2 * (pair + 1) * CHANNELS)
-            nc.sync.dma_start(out=x_raw[c, wr, side][:, tokens], in_=x_parts[2 * wr + c, side][:, :, tokens])
-
         def load_compressor(half):
             nc.sync.dma_start(
                 out=e_raw[:, half].rearrange("p c t l -> p c (t l)"),
@@ -138,11 +134,9 @@ def tile_efficientspatialwindowattention_pa_kernel(tc, x, kv_w, kv_b, E_k, E_v, 
                 in_=turned[:].rearrange("p j u t -> p j t u"),
             )
 
-        def quantise_tokens(part, pairs=(0, 2)):
-            words = slice(2 * P * pairs[0], 2 * P * pairs[1])
-            values = slice(PACK * 2 * P * pairs[0], PACK * 2 * P * pairs[1])
+        def quantise_tokens(part):
             nc.vector.quantize_mx(
-                out=x_codes[part][:, words].bitcast(FP8X4), scales=x_scales[part][:, words], in_=x_grouped[part][:, values]
+                out=x_codes[part][:].bitcast(FP8X4), scales=x_scales[part][:], in_=x_grouped[part][:]
             )
 
         def multiply_tokens(unit, head):
@@ -271,13 +265,11 @@ def tile_efficientspatialwindowattention_pa_kernel(tc, x, kv_w, kv_b, E_k, E_v, 
         nc.vector.memset(bias_row[:], 0.0)
         nc.vector.memset(ones[:], 1.0)
         make_identity(nc, identity[:])
-        for pair in range(2):
-            load_half_part(*parts[0], pair)
+        load_part(*parts[0])
         nc.sync.dma_start(out=bias_row[0:1, :], in_=kv_b.unsqueeze(0))
-        load_weights(0, PIECE)
-        load_weights(PIECE, PIECE)
-        load_part(*parts[1])
+        load_weights(0, HALF)
         load_weights(HALF, HALF)
+        load_part(*parts[1])
         load_compressor(0)
         load_part(*parts[2])
         load_part(*parts[3])
@@ -304,8 +296,7 @@ def tile_efficientspatialwindowattention_pa_kernel(tc, x, kv_w, kv_b, E_k, E_v, 
         group_weights(nc.vector.tensor_copy, 0, PIECE)
         group_weights(nc.scalar.copy, PIECE, PIECE)
         quantise_weights(0, PIECE)
-        quantise_tokens(parts[0], (0, 1))
-        quantise_tokens(parts[0], (1, 2))
+        quantise_tokens(parts[0])
 
         whole = slice(0, HALF)
         WE = [nc.vector.tensor_copy] * 4

@@ -218,8 +218,8 @@ def tile_efficientspatialwindowattention_pa_kernel(tc, x, kv_w, kv_b, E_k, E_v, 
         def group_compressor(half, m):
             for c in range(PASSES):
                 nc.scalar.copy(
-                    out=e_grouped[:, (half * ROW_TILES + m) * PASSES + c, :, :],
-                    in_=e_raw[:, half, c, :, :].rearrange("p t (n m) -> p m n t", m=ROW_TILES)[:, m],
+                    out=e_grouped[:, (half * ROW_TILES + m) * PASSES + c, :, :].rearrange("p (n i) t -> p n t i", i=4),
+                    in_=e_raw[:, half, c, :, m * P : (m + 1) * P].rearrange("p t (n i) -> p n t i", i=4),
                 )
 
         def quantise_compressor(half, m):
@@ -258,8 +258,8 @@ def tile_efficientspatialwindowattention_pa_kernel(tc, x, kv_w, kv_b, E_k, E_v, 
             copy(out=results[key][:, 0:heads, m, :], in_=out_bank[:, 0:heads, :])
             if m == ROW_TILES - 1:
                 nc.sync.dma_start(
-                    out=outs[half][2 * wr + side, first : first + heads].rearrange("h (n m) d -> n h (m d)", m=ROW_TILES),
-                    in_=results[key][:, 0:heads].rearrange("p h m d -> p h (m d)"),
+                    out=outs[half][2 * wr + side, first : first + heads].rearrange("h (m n) d -> n (h m) d", m=ROW_TILES),
+                    in_=results[key][:, 0:heads].rearrange("p h m d -> p (h m) d"),
                 )
 
         nc.vector.memset(bias_row[:], 0.0)
@@ -373,6 +373,6 @@ def tile_efficientspatialwindowattention_pa_kernel(tc, x, kv_w, kv_b, E_k, E_v, 
                 compress_pass(open_banks[k], wr, half, side, 2 * pair, 2, m, 1)
                 ENG[k](out=result[:, 0:2, m, :], in_=open_banks[k][:, 0:2, :])
             nc.sync.dma_start(
-                out=outs[half][2 * wr + side, 2 * pair : 2 * pair + 2].rearrange("h (n m) d -> n h (m d)", m=ROW_TILES),
-                in_=result[:, 0:2].rearrange("p h m d -> p h (m d)"),
+                out=outs[half][2 * wr + side, 2 * pair : 2 * pair + 2].rearrange("h (m n) d -> n (h m) d", m=ROW_TILES),
+                in_=result[:, 0:2].rearrange("p h m d -> p (h m) d"),
             )

@@ -28,6 +28,7 @@ TM = 2
 TURNED_UNITS = range(2, 16)
 WG = [(0, 0), (0, 1), (0, 2), (0, 3)]
 TILE0 = 9
+WARM = 20
 QP1 = (0, 2)
 QW1 = (1, 1)
 XB = 1
@@ -45,11 +46,12 @@ def tile_efficientspatialwindowattention_pa_kernel(tc, x, kv_w, kv_b, E_k, E_v, 
     with ExitStack() as ctx:
         keep = ctx.enter_context(tc.tile_pool(name="keep", bufs=1))
         x_stage = ctx.enter_context(tc.tile_pool(name="x_stage", bufs=4))
-        kv_stage = ctx.enter_context(tc.tile_pool(name="kv_stage", bufs=2))
+        kv_stage = ctx.enter_context(tc.tile_pool(name="kv_stage", bufs=3))
         turned_stage = ctx.enter_context(tc.tile_pool(name="turned_stage", bufs=2))
         out_stage = ctx.enter_context(tc.tile_pool(name="out_stage", bufs=4))
         turned_banks = ctx.enter_context(tc.psum_pool(name="turned_banks", bufs=2))
-        kv_banks = ctx.enter_context(tc.psum_pool(name="kv_banks", bufs=4))
+        channel_banks = ctx.enter_context(tc.psum_pool(name="channel_banks", bufs=1))
+        kv_banks = ctx.enter_context(tc.psum_pool(name="kv_banks", bufs=3))
         out_banks = ctx.enter_context(tc.psum_pool(name="out_banks", bufs=2))
         ctx.enter_context(tc.manual_schedule())
 
@@ -172,7 +174,7 @@ def tile_efficientspatialwindowattention_pa_kernel(tc, x, kv_w, kv_b, E_k, E_v, 
             c, wr, half, side = unit
             first = half * HALF + head * BLOCK
             cols = slice(first, first + BLOCK)
-            kv_bank = kv_banks.tile([P, 2, 2, P], F32, name="kv_bank")
+            kv_bank = channel_banks.tile([P, 2, 2, P], F32, name="channel_bank")
             nc.tensor.matmul_mx(
                 out=kv_bank[:].rearrange("n u e p -> n (u e p)"),
                 lhsT=w_codes[:, cols].bitcast(FP8X4),
@@ -262,8 +264,11 @@ def tile_efficientspatialwindowattention_pa_kernel(tc, x, kv_w, kv_b, E_k, E_v, 
                     in_=results[key][:, 0:heads].rearrange("p h m d -> p (h m) d"),
                 )
 
-        nc.vector.memset(bias_row[:], 0.0)
         nc.vector.memset(ones[:], 1.0)
+        nc.vector.memset(bias_row[:], 0.0)
+        nc.scalar.activation(
+            out=bias_column[:, 0, 0, 0:1], in_=ones[:, 0:1], func=mybir.ActivationFunctionType.Identity
+        )
         make_identity(nc, identity[:])
         load_part(*parts[0])
         nc.sync.dma_start(out=bias_row[0:1, :], in_=kv_b.unsqueeze(0))
@@ -277,6 +282,9 @@ def tile_efficientspatialwindowattention_pa_kernel(tc, x, kv_w, kv_b, E_k, E_v, 
         for part in parts[4:]:
             load_part(*part)
 
+        warm = out_banks.tile([P, P], F32, tag="out_bank")
+        for i in range(WARM):
+            nc.tensor.matmul(out=warm[:], lhsT=ones[:], rhs=ones[:], start=True, stop=True)
         for pair in range(2):
             turn_tokens(parts[0], pair)
         for half in range(2):
@@ -314,6 +322,7 @@ def tile_efficientspatialwindowattention_pa_kernel(tc, x, kv_w, kv_b, E_k, E_v, 
 
         KV = (kv_banks, "kv_bank")
         TU = (turned_banks, "turned")
+        CH = (channel_banks, "channel_bank")
         A, V = nc.scalar.copy, nc.vector.tensor_copy
         ENG = [A, A, A, V, A, V]
         new_grouped(units[0])
@@ -360,7 +369,7 @@ def tile_efficientspatialwindowattention_pa_kernel(tc, x, kv_w, kv_b, E_k, E_v, 
         last = units[-1]
         quantise_unit(last, slice(PIECE, HALF))
         wr, side, half = groups[-1][0], groups[-1][2], groups[-1][1]
-        last_banks = [TU, TU, KV, KV, KV, KV]
+        last_banks = [TU, TU, KV, KV, KV, CH]
         open_banks = {}
         for k in range(2 * ROW_TILES):
             pool, tag = last_banks[k]

@@ -64,13 +64,13 @@ def tile_efficientspatialwindowattention_pa_kernel(tc, x, kv_w, kv_b, E_k, E_v, 
         bias_all = keep.tile([P, 2 * HALF], F32)
         bias_column = keep.tile([P, 2, HEADS, 2], F32)
         w_raw = keep.tile([P, PACK, 2 * HALF], BF16)
-        w_grouped = keep.tile([P, 2 * HALF, PACK], BF16, align_bytes=64)
-        w_codes = keep.tile([P, 2 * HALF], U32, align_bytes=64)
-        w_scales = keep.tile([P, 2 * HALF], U8, align_bytes=64)
+        w_grouped = keep.tile([P, 2 * HALF, PACK], BF16, align_bytes=256)
+        w_codes = keep.tile([P, 2 * HALF], U32, align_bytes=256)
+        w_scales = keep.tile([P, 2 * HALF], U8, align_bytes=256)
         e_raw = keep.tile([P, 2, PASSES, PACK, LK], BF16)
-        e_grouped = keep.tile([P, E_TILES, P, PACK], BF16, align_bytes=64)
-        e_codes = keep.tile([P, E_TILES, P], U32, align_bytes=64)
-        e_scales = keep.tile([P, E_TILES, P], U8, align_bytes=64)
+        e_grouped = keep.tile([P, E_TILES, P, PACK], BF16, align_bytes=256)
+        e_codes = keep.tile([P, E_TILES, P], U32, align_bytes=256)
+        e_scales = keep.tile([P, E_TILES, P], U8, align_bytes=256)
         x_raw = {}
         x_grouped = {}
         x_codes = {}
@@ -78,8 +78,8 @@ def tile_efficientspatialwindowattention_pa_kernel(tc, x, kv_w, kv_b, E_k, E_v, 
         for part in parts:
             tail = "_%d%d%d" % part
             x_raw[part] = keep.tile([P, PACK * CHANNELS], BF16, name="x_raw" + tail)
-            x_codes[part] = keep.tile([P, PACK * P], U32, name="x_codes" + tail, align_bytes=64)
-            x_scales[part] = keep.tile([P, PACK * P], U8, name="x_scales" + tail, align_bytes=64)
+            x_codes[part] = keep.tile([P, PACK * P], U32, name="x_codes" + tail, align_bytes=256)
+            x_scales[part] = keep.tile([P, PACK * P], U8, name="x_scales" + tail, align_bytes=256)
         kv_grouped = {}
         kv_turned = {}
         results = {}
@@ -87,8 +87,8 @@ def tile_efficientspatialwindowattention_pa_kernel(tc, x, kv_w, kv_b, E_k, E_v, 
         kv_scales = {}
         for unit in units:
             tail = "_%d%d%d%d" % unit
-            kv_codes[unit] = keep.tile([P, HALF], U32, name="kv_codes" + tail, align_bytes=64)
-            kv_scales[unit] = keep.tile([P, HALF], U8, name="kv_scales" + tail, align_bytes=64)
+            kv_codes[unit] = keep.tile([P, HALF], U32, name="kv_codes" + tail, align_bytes=256)
+            kv_scales[unit] = keep.tile([P, HALF], U8, name="kv_scales" + tail, align_bytes=256)
 
         def load_weights(first, width):
             cols = slice(first, first + width)
@@ -124,7 +124,7 @@ def tile_efficientspatialwindowattention_pa_kernel(tc, x, kv_w, kv_b, E_k, E_v, 
 
         def turn_tokens(part, pair):
             if pair == 0:
-                x_grouped[part] = x_stage.tile([P, PACK * P * PACK], BF16, name="x_grouped", align_bytes=64)
+                x_grouped[part] = x_stage.tile([P, PACK * P * PACK], BF16, name="x_grouped", align_bytes=256)
             turned = turned_banks.tile([P, 2, 2, P], F32, tag="turned")
             words = x_raw[part][:].bitcast(F32)
             for j in range(2):
@@ -221,7 +221,7 @@ def tile_efficientspatialwindowattention_pa_kernel(tc, x, kv_w, kv_b, E_k, E_v, 
             for c in range(PASSES):
                 nc.scalar.copy(
                     out=e_grouped[:, (half * ROW_TILES + m) * PASSES + c, :, :].rearrange("p (n i) t -> p n t i", i=4),
-                    in_=e_raw[:, half, c, :, m * P : (m + 1) * P].rearrange("p t (n i) -> p n t i", i=4),
+                    in_=e_raw[:, half, c, :, :].rearrange("p t (n i m) -> p m n t i", i=4, m=ROW_TILES)[:, m],
                 )
 
         def quantise_compressor(half, m):
@@ -260,8 +260,8 @@ def tile_efficientspatialwindowattention_pa_kernel(tc, x, kv_w, kv_b, E_k, E_v, 
             copy(out=results[key][:, 0:heads, m, :], in_=out_bank[:, 0:heads, :])
             if m == ROW_TILES - 1:
                 nc.sync.dma_start(
-                    out=outs[half][2 * wr + side, first : first + heads].rearrange("h (m n) d -> n (h m) d", m=ROW_TILES),
-                    in_=results[key][:, 0:heads].rearrange("p h m d -> p (h m) d"),
+                    out=outs[half][2 * wr + side, first : first + heads].rearrange("h (n m) d -> n h (m d)", m=ROW_TILES),
+                    in_=results[key][:, 0:heads].rearrange("p h m d -> p h (m d)"),
                 )
 
         nc.vector.memset(ones[:], 1.0)
@@ -318,7 +318,7 @@ def tile_efficientspatialwindowattention_pa_kernel(tc, x, kv_w, kv_b, E_k, E_v, 
         e_pairs = [(half, m) for half in range(2) for m in range(ROW_TILES)]
 
         def new_grouped(unit):
-            kv_grouped[unit] = kv_stage.tile([P, HALF, PACK], BF16, name="kv_grouped", align_bytes=64)
+            kv_grouped[unit] = kv_stage.tile([P, HALF, PACK], BF16, name="kv_grouped", align_bytes=256)
 
         KV = (kv_banks, "kv_bank")
         TU = (turned_banks, "turned")
@@ -382,6 +382,6 @@ def tile_efficientspatialwindowattention_pa_kernel(tc, x, kv_w, kv_b, E_k, E_v, 
                 compress_pass(open_banks[k], wr, half, side, 2 * pair, 2, m, 1)
                 ENG[k](out=result[:, 0:2, m, :], in_=open_banks[k][:, 0:2, :])
             nc.sync.dma_start(
-                out=outs[half][2 * wr + side, 2 * pair : 2 * pair + 2].rearrange("h (m n) d -> n (h m) d", m=ROW_TILES),
-                in_=result[:, 0:2].rearrange("p h m d -> p (h m) d"),
+                out=outs[half][2 * wr + side, 2 * pair : 2 * pair + 2].rearrange("h (n m) d -> n h (m d)", m=ROW_TILES),
+                in_=result[:, 0:2].rearrange("p h m d -> p h (m d)"),
             )

@@ -25,6 +25,10 @@ HEADS = 4
 E_START = 0
 TURNED = 3
 TM = 2
+TBP = 1
+BU = [max(1, j - 1) for j in range(12)]
+QE = 0
+QT = 2
 TURNED_UNITS = range(2, 16)
 WG = [(0, 0), (0, 1), (0, 2), (0, 3)]
 TILE0 = 9
@@ -273,8 +277,8 @@ def tile_efficientspatialwindowattention_pa_kernel(tc, x, kv_w, kv_b, E_k, E_v, 
         load_part(*parts[0])
         nc.sync.dma_start(out=bias_row[0:1, :], in_=kv_b.unsqueeze(0))
         load_weights(0, HALF)
-        load_weights(HALF, HALF)
         load_part(*parts[1])
+        load_weights(HALF, HALF)
         load_compressor(0)
         load_part(*parts[2])
         load_part(*parts[3])
@@ -309,7 +313,7 @@ def tile_efficientspatialwindowattention_pa_kernel(tc, x, kv_w, kv_b, E_k, E_v, 
         whole = slice(0, HALF)
         WE = [nc.vector.tensor_copy] * 4
         later_banks = [(part, pair) for part in parts[1:] for pair in range(2)]
-        bank_unit = [0, 0] + [max(1, j // 2) if j < 4 else j - 1 for j in range(2 * len(parts) - 4)]
+        bank_unit = [0, 0] + BU
         slots = {}
         groups = [(wr, half, side) for wr in range(2) for side in range(2) for half in range(2)]
         tiles = [(*group, 0, HEADS, m) for group in groups[:-1] for m in range(ROW_TILES)]
@@ -332,13 +336,14 @@ def tile_efficientspatialwindowattention_pa_kernel(tc, x, kv_w, kv_b, E_k, E_v, 
             ready = [k[0] for k, u in zip(later_banks, bank_unit) if u == s - 1 and k[1] == 1 and k[0] != parts[1]]
             for b in blocks:
                 project(unit, b)
-                if b == 0:
-                    if 0 <= s - 1 - E_START < len(e_pairs):
-                        quantise_compressor(*e_pairs[s - 1 - E_START])
-                    if s == 0:
-                        quantise_weights(PIECE, PIECE)
+                if b == QE and 0 <= s - 1 - E_START < len(e_pairs):
+                    quantise_compressor(*e_pairs[s - 1 - E_START])
+                if b == QT:
                     for part in ready:
                         quantise_tokens(part)
+                if b == 0:
+                    if s == 0:
+                        quantise_weights(PIECE, PIECE)
                     if 1 <= s < len(units) - 1:
                         quantise_unit(units[s - 1], whole)
                 if b == 0:
@@ -350,8 +355,8 @@ def tile_efficientspatialwindowattention_pa_kernel(tc, x, kv_w, kv_b, E_k, E_v, 
                 if b == XB:
                     for bank in banks:
                         turn_tokens(*bank)
-                    if s in TURNED_UNITS:
-                        turn_back(unit, [TURNED])
+                if b == TBP and s in TURNED_UNITS:
+                    turn_back(unit, [TURNED])
                 if b == TM and s + 1 in TURNED_UNITS:
                     project_turned(units[s + 1], TURNED)
                 if b == EB and 0 <= s - E_START < len(e_pairs):

@@ -25,6 +25,7 @@ HEADS = 4
 E_START = 0
 TURNED = 3
 TM = 2
+LS = 44
 TBP = 1
 BU = [max(1, j - 1) for j in range(12)]
 QE = 0
@@ -277,8 +278,8 @@ def tile_efficientspatialwindowattention_pa_kernel(tc, x, kv_w, kv_b, E_k, E_v, 
         load_part(*parts[0])
         nc.sync.dma_start(out=bias_row[0:1, :], in_=kv_b.unsqueeze(0))
         load_weights(0, HALF)
-        load_part(*parts[1])
         load_weights(HALF, HALF)
+        load_part(*parts[1])
         load_compressor(0)
         load_part(*parts[2])
         load_part(*parts[3])
@@ -318,7 +319,7 @@ def tile_efficientspatialwindowattention_pa_kernel(tc, x, kv_w, kv_b, E_k, E_v, 
         groups = [(wr, half, side) for wr in range(2) for side in range(2) for half in range(2)]
         tiles = [(*group, 0, HEADS, m) for group in groups[:-1] for m in range(ROW_TILES)]
         for i, tile in enumerate(tiles):
-            slots.setdefault(min(3 * len(units) - 1, TILE0 + 2 * i), []).append(tile)
+            slots.setdefault(TILE0 + 2 * i if i < 18 else LS + i - 18, []).append(tile)
         e_pairs = [(half, m) for half in range(2) for m in range(ROW_TILES)]
 
         def new_grouped(unit):
@@ -328,7 +329,6 @@ def tile_efficientspatialwindowattention_pa_kernel(tc, x, kv_w, kv_b, E_k, E_v, 
         TU = (turned_banks, "turned")
         CH = (channel_banks, "channel_bank")
         A, V = nc.scalar.copy, nc.vector.tensor_copy
-        ENG = [A, A, A, V, A, V]
         new_grouped(units[0])
         for s, unit in enumerate(units):
             blocks = range(TURNED if s in TURNED_UNITS else HEADS)
@@ -371,22 +371,26 @@ def tile_efficientspatialwindowattention_pa_kernel(tc, x, kv_w, kv_b, E_k, E_v, 
                 if b == 1 and s == len(units) - 1:
                     quantise_unit(units[s - 1], whole)
                     quantise_unit(unit, slice(0, PIECE))
+                    quantise_unit(unit, slice(TURNED * BLOCK, HALF))
         last = units[-1]
-        quantise_unit(last, slice(PIECE, HALF))
-        wr, side, half = groups[-1][0], groups[-1][2], groups[-1][1]
-        last_banks = [TU, TU, KV, KV, KV, CH]
-        open_banks = {}
-        for k in range(2 * ROW_TILES):
-            pool, tag = last_banks[k]
-            open_banks[k] = pool.tile([P, HEADS, BLOCK], F32, name="open_bank", tag=tag)
-            compress_pass(open_banks[k], wr, half, side, 2 * (k // ROW_TILES), 2, k % ROW_TILES, 0)
-        for pair in range(2):
+        quantise_unit(last, slice(PIECE, TURNED * BLOCK))
+        wr, half, side = groups[-1]
+        for first, heads, banks, copies in [
+            (0, 2, [TU, TU, KV], [A, A, A]),
+            (TURNED, 1, [KV, KV, CH], [A, A, A]),
+            (2, 1, [TU, TU, KV], [V, A, V]),
+        ]:
+            tiles = []
+            for m in range(ROW_TILES):
+                pool, tag = banks[m]
+                open_bank = pool.tile([P, HEADS, BLOCK], F32, name="open_bank", tag=tag)
+                compress_pass(open_bank, wr, half, side, first, heads, m, 0)
+                tiles.append(open_bank)
             result = out_stage.tile([P, HEADS, ROW_TILES, BLOCK], F32, name="result")
             for m in range(ROW_TILES):
-                k = ROW_TILES * pair + m
-                compress_pass(open_banks[k], wr, half, side, 2 * pair, 2, m, 1)
-                ENG[k](out=result[:, 0:2, m, :], in_=open_banks[k][:, 0:2, :])
+                compress_pass(tiles[m], wr, half, side, first, heads, m, 1)
+                copies[m](out=result[:, 0:heads, m, :], in_=tiles[m][:, 0:heads, :])
             nc.sync.dma_start(
-                out=outs[half][2 * wr + side, 2 * pair : 2 * pair + 2].rearrange("h (n m) d -> n h (m d)", m=ROW_TILES),
-                in_=result[:, 0:2].rearrange("p h m d -> p h (m d)"),
+                out=outs[half][2 * wr + side, first : first + heads].rearrange("h (n m) d -> n h (m d)", m=ROW_TILES),
+                in_=result[:, 0:heads].rearrange("p h m d -> p h (m d)"),
             )

@@ -31,11 +31,11 @@ BU = [max(1, j - 1) for j in range(12)]
 QE = 0
 QT = 2
 TURNED_UNITS = range(2, 16)
-WG = [(0, 0), (0, 1), (0, 2), (0, 3)]
+WG = [(0, 0), (0, 1), (0, 3), (0, 3)]
 TILE0 = 9
 WARM = 20
 QP1 = (0, 2)
-QW1 = (1, 1)
+QW1 = (1, 0)
 XB = 1
 EB = 1
 
@@ -276,8 +276,8 @@ def tile_efficientspatialwindowattention_pa_kernel(tc, x, kv_w, kv_b, E_k, E_v, 
         )
         make_identity(nc, identity[:])
         load_part(*parts[0])
-        nc.sync.dma_start(out=bias_row[0:1, :], in_=kv_b.unsqueeze(0))
         load_weights(0, HALF)
+        nc.sync.dma_start(out=bias_row[0:1, :], in_=kv_b.unsqueeze(0))
         load_weights(HALF, HALF)
         load_part(*parts[1])
         load_compressor(0)
@@ -308,8 +308,8 @@ def tile_efficientspatialwindowattention_pa_kernel(tc, x, kv_w, kv_b, E_k, E_v, 
 
         group_weights(nc.vector.tensor_copy, 0, PIECE)
         group_weights(nc.scalar.copy, PIECE, PIECE)
-        quantise_weights(0, PIECE)
         quantise_tokens(parts[0])
+        quantise_weights(0, PIECE)
 
         whole = slice(0, HALF)
         WE = [nc.vector.tensor_copy] * 4

@@ -30,7 +30,7 @@ TBP = 1
 BU = [max(1, j - 1) for j in range(12)]
 QE = 0
 QT = 2
-TURNED_UNITS = range(2, 16)
+TURNED_UNITS = range(2, 14)
 WG = [(0, 0), (0, 1), (0, 3), (0, 3)]
 TILE0 = 9
 WARM = 20
@@ -98,7 +98,7 @@ def tile_efficientspatialwindowattention_pa_kernel(tc, x, kv_w, kv_b, E_k, E_v, 
         def load_weights(first, width):
             cols = slice(first, first + width)
             for u in range(2):
-                nc.sync.dma_start(
+                nc.scalar.dma_start(
                     out=w_raw[:, 2 * u : 2 * u + 2, cols],
                     in_=kv_w[2 * P * u : 2 * P * (u + 1), cols].rearrange("(q e) n -> q e n", e=2),
                 )
@@ -277,8 +277,8 @@ def tile_efficientspatialwindowattention_pa_kernel(tc, x, kv_w, kv_b, E_k, E_v, 
         make_identity(nc, identity[:])
         load_part(*parts[0])
         load_weights(0, HALF)
-        nc.sync.dma_start(out=bias_row[0:1, :], in_=kv_b.unsqueeze(0))
         load_weights(HALF, HALF)
+        nc.sync.dma_start(out=bias_row[0:1, :], in_=kv_b.unsqueeze(0))
         load_part(*parts[1])
         load_compressor(0)
         load_part(*parts[2])
@@ -371,14 +371,14 @@ def tile_efficientspatialwindowattention_pa_kernel(tc, x, kv_w, kv_b, E_k, E_v, 
                 if b == 1 and s == len(units) - 1:
                     quantise_unit(units[s - 1], whole)
                     quantise_unit(unit, slice(0, PIECE))
-                    quantise_unit(unit, slice(TURNED * BLOCK, HALF))
         last = units[-1]
-        quantise_unit(last, slice(PIECE, TURNED * BLOCK))
+        for head in range(2, HEADS):
+            quantise_unit(last, slice(head * BLOCK, (head + 1) * BLOCK))
         wr, half, side = groups[-1]
         for first, heads, banks, copies in [
             (0, 2, [TU, TU, KV], [A, A, A]),
-            (TURNED, 1, [KV, KV, CH], [A, A, A]),
-            (2, 1, [TU, TU, KV], [V, A, V]),
+            (2, 1, [KV, KV, CH], [A, A, A]),
+            (3, 1, [TU, TU, KV], [V, A, V]),
         ]:
             tiles = []
             for m in range(ROW_TILES):

from contextlib import ExitStack

import concourse.mybir as mybir
from concourse.masks import make_identity

F32 = mybir.dt.float32
BF16 = mybir.dt.bfloat16
U32 = mybir.dt.uint32
U8 = mybir.dt.uint8
FP8X4 = mybir.dt.float8_e4m3fn_x4

P = 128
PACK = 4
CHANNELS = 512
HALF = 512
PIECE = 256
BLOCK = 128
LK = 384
ROW_TILES = LK // P
PASSES = 2
E_TILES = 2 * PASSES * ROW_TILES
BAND_ROWS = 16
GROUPS = 8
HEADS = 4
E_START = 0
TURNED = 3
TM = 2
LS = 44
TBP = 1
BU = [max(1, j - 1) for j in range(12)]
QE = 0
QT = 2
TURNED_UNITS = range(2, 14)
WG = [(0, 0), (0, 1), (0, 3), (0, 3)]
TILE0 = 9
WARM = 20
QP1 = (0, 2)
QW1 = (1, 0)
XB = 1
EB = 1

FLOPS = 2 * 4096 * 512 * 1024 + 2 * 2 * 4 * 384 * 1024 * 512


def tile_efficientspatialwindowattention_pa_kernel(tc, x, kv_w, kv_b, E_k, E_v, out_0, out_1):
    nc = tc.nc
    outs = [out_0, out_1]
    compressors = [E_k, E_v]
    x_parts = x.rearrange("o (b r w g j) ch -> (o b) w r g (j ch)", b=4, r=BAND_ROWS, w=2, g=GROUPS)

    with ExitStack() as ctx:
        keep = ctx.enter_context(tc.tile_pool(name="keep", bufs=1))
        x_stage = ctx.enter_context(tc.tile_pool(name="x_stage", bufs=4))
        kv_stage = ctx.enter_context(tc.tile_pool(name="kv_stage", bufs=3))
        turned_stage = ctx.enter_context(tc.tile_pool(name="turned_stage", bufs=2))
        out_stage = ctx.enter_context(tc.tile_pool(name="out_stage", bufs=4))
        turned_banks = ctx.enter_context(tc.psum_pool(name="turned_banks", bufs=2))
        channel_banks = ctx.enter_context(tc.psum_pool(name="channel_banks", bufs=1))
        kv_banks = ctx.enter_context(tc.psum_pool(name="kv_banks", bufs=3))
        out_banks = ctx.enter_context(tc.psum_pool(name="out_banks", bufs=2))
        ctx.enter_context(tc.manual_schedule())

        parts = [(c, wr, side) for wr in range(2) for side in range(2) for c in range(PASSES)]
        units = [(c, wr, half, side) for wr in range(2) for side in range(2) for half in range(2) for c in range(PASSES)]

        identity = keep.tile([P, P], F32)
        ones = keep.tile([P, P], BF16)
        bias_row = keep.tile([P, 2 * HALF], BF16)
        bias_all = keep.tile([P, 2 * HALF], F32)
        bias_column = keep.tile([P, 2, HEADS, 2], F32)
        w_raw = keep.tile([P, PACK, 2 * HALF], BF16)
        w_grouped = keep.tile([P, 2 * HALF, PACK], BF16, align_bytes=256)
        w_codes = keep.tile([P, 2 * HALF], U32, align_bytes=256)
        w_scales = keep.tile([P, 2 * HALF], U8, align_bytes=256)
        e_raw = keep.tile([P, 2, PASSES, PACK, LK], BF16)
        e_grouped = keep.tile([P, E_TILES, P, PACK], BF16, align_bytes=256)
        e_codes = keep.tile([P, E_TILES, P], U32, align_bytes=256)
        e_scales = keep.tile([P, E_TILES, P], U8, align_bytes=256)
        x_raw = {}
        x_grouped = {}
        x_codes = {}
        x_scales = {}
        for part in parts:
            tail = "_%d%d%d" % part
            x_raw[part] = keep.tile([P, PACK * CHANNELS], BF16, name="x_raw" + tail)
            x_codes[part] = keep.tile([P, PACK * P], U32, name="x_codes" + tail, align_bytes=256)
            x_scales[part] = keep.tile([P, PACK * P], U8, name="x_scales" + tail, align_bytes=256)
        kv_grouped = {}
        kv_turned = {}
        results = {}
        kv_codes = {}
        kv_scales = {}
        for unit in units:
            tail = "_%d%d%d%d" % unit
            kv_codes[unit] = keep.tile([P, HALF], U32, name="kv_codes" + tail, align_bytes=256)
            kv_scales[unit] = keep.tile([P, HALF], U8, name="kv_scales" + tail, align_bytes=256)

        def load_weights(first, width):
            cols = slice(first, first + width)
            for u in range(2):
                nc.scalar.dma_start(
                    out=w_raw[:, 2 * u : 2 * u + 2, cols],
                    in_=kv_w[2 * P * u : 2 * P * (u + 1), cols].rearrange("(q e) n -> q e n", e=2),
                )

        def load_part(c, wr, side):
            nc.sync.dma_start(out=x_raw[c, wr, side][:], in_=x_parts[2 * wr + c, side])

        def load_compressor(half):
            nc.sync.dma_start(
                out=e_raw[:, half].rearrange("p c t l -> p c (t l)"),
                in_=compressors[half].rearrange("(c p t) l -> p c (t l)", c=PASSES, t=PACK),
            )

        def group_weights(copy, first, width):
            cols = slice(first, first + width)
            copy(
                out=w_grouped[:, cols, :].rearrange("p (n i) t -> p n t i", i=4),
                in_=w_raw[:, :, cols].rearrange("p t (n i) -> p n t i", i=4),
            )

        def quantise_weights(first, width):
            cols = slice(first, first + width)
            nc.vector.quantize_mx(
                out=w_codes[:, cols].bitcast(FP8X4),
                scales=w_scales[:, cols],
                in_=w_grouped[:, cols, :].rearrange("p n t -> p (n t)"),
            )

        def turn_tokens(part, pair):
            if pair == 0:
                x_grouped[part] = x_stage.tile([P, PACK * P * PACK], BF16, name="x_grouped", align_bytes=256)
            turned = turned_banks.tile([P, 2, 2, P], F32, tag="turned")
            words = x_raw[part][:].bitcast(F32)
            for j in range(2):
                for u in range(2):
                    first = (2 * (2 * pair + j) + u) * P
                    nc.tensor.transpose(turned[:, j, u, :], words[:, first : first + P], identity[:])
            nc.scalar.copy(
                out=x_grouped[part][:].bitcast(F32).rearrange("p (a j t u) -> p a j t u", a=2, j=2, u=2)[:, pair],
                in_=turned[:].rearrange("p j u t -> p j t u"),
            )

        def quantise_tokens(part):
            nc.vector.quantize_mx(
                out=x_codes[part][:].bitcast(FP8X4), scales=x_scales[part][:], in_=x_grouped[part][:]
            )

        def multiply_tokens(unit, head):
            c, wr, half, side = unit
            first = half * HALF + head * BLOCK
            cols = slice(first, first + BLOCK)
            kv_bank = kv_banks.tile([P, PACK, BLOCK], F32, name="kv_bank")
            for j in range(PACK):
                tokens = slice(j * P, (j + 1) * P)
                nc.tensor.matmul_mx(
                    out=kv_bank[:, j, :],
                    lhsT=x_codes[c, wr, side][:, tokens].bitcast(FP8X4),
                    lhsT_scale=x_scales[c, wr, side][:, tokens],
                    rhs=w_codes[:, cols].bitcast(FP8X4),
                    rhs_scale=w_scales[:, cols],
                    start=True,
                    stop=True,
                )
            return kv_bank

        def project(unit, block):
            first = unit[2] * HALF + block * BLOCK
            cols = slice(first, first + BLOCK)
            kv_bank = multiply_tokens(unit, block)
            nc.vector.tensor_tensor(
                out=kv_grouped[unit][:, block * BLOCK : (block + 1) * BLOCK, :],
                in0=kv_bank[:].rearrange("p j n -> p n j"),
                in1=bias_all[:, cols].unsqueeze(2).to_broadcast([P, BLOCK, PACK]),
                op=mybir.AluOpType.add,
            )

        def project_turned(unit, head):
            c, wr, half, side = unit
            first = half * HALF + head * BLOCK
            cols = slice(first, first + BLOCK)
            kv_bank = channel_banks.tile([P, 2, 2, P], F32, name="channel_bank")
            nc.tensor.matmul_mx(
                out=kv_bank[:].rearrange("n u e p -> n (u e p)"),
                lhsT=w_codes[:, cols].bitcast(FP8X4),
                lhsT_scale=w_scales[:, cols],
                rhs=x_codes[c, wr, side][:].bitcast(FP8X4),
                rhs_scale=x_scales[c, wr, side][:],
                start=True,
                stop=True,
            )
            kv_turned[unit, head] = turned_stage.tile([P, 2, P, 2], BF16, name="kv_turned")
            nc.scalar.activation(
                out=kv_turned[unit, head][:],
                in_=kv_bank[:].rearrange("n u e p -> n u p e"),
                func=mybir.ActivationFunctionType.Identity,
                bias=bias_column[:, half, head, 0:1],
            )

        def turn_back(unit, heads):
            back = turned_banks.tile([P, 2, 2, BLOCK], F32, tag="turned")
            count = len(heads)
            for h, head in enumerate(heads):
                for u in range(2):
                    nc.tensor.transpose(
                        back[:, h, u, :],
                        kv_turned[unit, head][:, u].rearrange("n p e -> n (p e)").bitcast(F32),
                        identity[:],
                    )
            nc.scalar.copy(
                out=kv_grouped[unit][:, heads[0] * BLOCK : (heads[0] + count) * BLOCK, :]
                .rearrange("p n j -> p (n j)")
                .bitcast(F32)
                .rearrange("p (h n u) -> p h n u", h=count, u=2),
                in_=back[:, 0:count].rearrange("p h u n -> p h n u"),
            )

        def quantise_unit(unit, cols):
            nc.vector.quantize_mx(
                out=kv_codes[unit][:, cols].bitcast(FP8X4),
                scales=kv_scales[unit][:, cols],
                in_=kv_grouped[unit][:, cols, :].rearrange("p n j -> p (n j)"),
            )

        def group_compressor(half, m):
            for c in range(PASSES):
                nc.scalar.copy(
                    out=e_grouped[:, (half * ROW_TILES + m) * PASSES + c, :, :].rearrange("p (n i) t -> p n t i", i=4),
                    in_=e_raw[:, half, c, :, :].rearrange("p t (n i m) -> p m n t i", i=4, m=ROW_TILES)[:, m],
                )

        def quantise_compressor(half, m):
            first = (half * ROW_TILES + m) * PASSES
            tiles = slice(first, first + PASSES)
            nc.vector.quantize_mx(
                out=e_codes[:, tiles, :].rearrange("p e n -> p (e n)").bitcast(FP8X4),
                scales=e_scales[:, tiles, :].rearrange("p e n -> p (e n)"),
                in_=e_grouped[:, tiles, :, :].rearrange("p e n t -> p (e n t)"),
            )

        def compress_pass(out_bank, wr, half, side, first, heads, m, c):
            e = (half * ROW_TILES + m) * PASSES + c
            cols = slice(first * BLOCK, (first + heads) * BLOCK)
            nc.tensor.matmul_mx(
                out=out_bank[:, 0:heads, :].rearrange("p h d -> p (h d)"),
                lhsT=e_codes[:, e, :].bitcast(FP8X4),
                lhsT_scale=e_scales[:, e, :],
                rhs=kv_codes[c, wr, half, side][:, cols].bitcast(FP8X4),
                rhs_scale=kv_scales[c, wr, half, side][:, cols],
                start=(c == 0),
                stop=(c == PASSES - 1),
            )

        def compress(wr, half, side, first, heads, m, copy=nc.scalar.copy, banks=None):
            key = (wr, half, side, first)
            if m == 0:
                results[key] = out_stage.tile([P, HEADS, ROW_TILES, BLOCK], F32, name="result")
            cols = slice(first * BLOCK, (first + heads) * BLOCK)
            if banks is None:
                out_bank = out_banks.tile([P, HEADS, BLOCK], F32, tag="out_bank")
            else:
                out_bank = banks[0].tile([P, HEADS, BLOCK], F32, tag=banks[1])
            for c in range(PASSES):
                compress_pass(out_bank, wr, half, side, first, heads, m, c)
            copy(out=results[key][:, 0:heads, m, :], in_=out_bank[:, 0:heads, :])
            if m == ROW_TILES - 1:
                nc.sync.dma_start(
                    out=outs[half][2 * wr + side, first : first + heads].rearrange("h (n m) d -> n h (m d)", m=ROW_TILES),
                    in_=results[key][:, 0:heads].rearrange("p h m d -> p h (m d)"),
                )

        nc.vector.memset(ones[:], 1.0)
        nc.vector.memset(bias_row[:], 0.0)
        nc.scalar.activation(
            out=bias_column[:, 0, 0, 0:1], in_=ones[:, 0:1], func=mybir.ActivationFunctionType.Identity
        )
        make_identity(nc, identity[:])
        load_part(*parts[0])
        load_weights(0, HALF)
        load_weights(HALF, HALF)
        nc.sync.dma_start(out=bias_row[0:1, :], in_=kv_b.unsqueeze(0))
        load_part(*parts[1])
        load_compressor(0)
        load_part(*parts[2])
        load_part(*parts[3])
        load_compressor(1)
        for part in parts[4:]:
            load_part(*part)

        warm = out_banks.tile([P, P], F32, tag="out_bank")
        for i in range(WARM):
            nc.tensor.matmul(out=warm[:], lhsT=ones[:], rhs=ones[:], start=True, stop=True)
        for pair in range(2):
            turn_tokens(parts[0], pair)
        for half in range(2):
            cols = slice(half * HALF, (half + 1) * HALF)
            spread = out_banks.tile([P, HALF], F32, tag="out_bank")
            nc.tensor.matmul(out=spread[:], lhsT=ones[:], rhs=bias_row[:, cols], start=True, stop=True)
            nc.scalar.copy(out=bias_all[:, cols], in_=spread[:])
        column = out_banks.tile([P, 2, HEADS, 2], F32, tag="out_bank")
        for half in range(2):
            for head in range(TURNED, HEADS):
                first = half * HALF + head * BLOCK
                nc.tensor.matmul(
                    out=column[:, half, head, :], lhsT=bias_row[:, first : first + BLOCK], rhs=ones[:, 0:2], start=True, stop=True
                )
        nc.scalar.copy(out=bias_column[:, :, TURNED:HEADS], in_=column[:, :, TURNED:HEADS])

        group_weights(nc.vector.tensor_copy, 0, PIECE)
        group_weights(nc.scalar.copy, PIECE, PIECE)
        quantise_tokens(parts[0])
        quantise_weights(0, PIECE)

        whole = slice(0, HALF)
        WE = [nc.vector.tensor_copy] * 4
        later_banks = [(part, pair) for part in parts[1:] for pair in range(2)]
        bank_unit = [0, 0] + BU
        slots = {}
        groups = [(wr, half, side) for wr in range(2) for side in range(2) for half in range(2)]
        tiles = [(*group, 0, HEADS, m) for group in groups[:-1] for m in range(ROW_TILES)]
        for i, tile in enumerate(tiles):
            slots.setdefault(TILE0 + 2 * i if i < 18 else LS + i - 18, []).append(tile)
        e_pairs = [(half, m) for half in range(2) for m in range(ROW_TILES)]

        def new_grouped(unit):
            kv_grouped[unit] = kv_stage.tile([P, HALF, PACK], BF16, name="kv_grouped", align_bytes=256)

        KV = (kv_banks, "kv_bank")
        TU = (turned_banks, "turned")
        CH = (channel_banks, "channel_bank")
        A, V = nc.scalar.copy, nc.vector.tensor_copy
        new_grouped(units[0])
        for s, unit in enumerate(units):
            blocks = range(TURNED if s in TURNED_UNITS else HEADS)
            banks = [k for k, u in zip(later_banks, bank_unit) if u == s]
            ready = [k[0] for k, u in zip(later_banks, bank_unit) if u == s - 1 and k[1] == 1 and k[0] != parts[1]]
            for b in blocks:
                project(unit, b)
                if b == QE and 0 <= s - 1 - E_START < len(e_pairs):
                    quantise_compressor(*e_pairs[s - 1 - E_START])
                if b == QT:
                    for part in ready:
                        quantise_tokens(part)
                if b == 0:
                    if s == 0:
                        quantise_weights(PIECE, PIECE)
                    if 1 <= s < len(units) - 1:
                        quantise_unit(units[s - 1], whole)
                if b == 0:
                    if s + 1 < len(units):
                        new_grouped(units[s + 1])
                for k in range(4):
                    if (s, b) == WG[k]:
                        group_weights(WE[k], HALF + k * BLOCK, BLOCK)
                if b == XB:
                    for bank in banks:
                        turn_tokens(*bank)
                if b == TBP and s in TURNED_UNITS:
                    turn_back(unit, [TURNED])
                if b == TM and s + 1 in TURNED_UNITS:
                    project_turned(units[s + 1], TURNED)
                if b == EB and 0 <= s - E_START < len(e_pairs):
                    group_compressor(*e_pairs[s - E_START])
                if (s, b) == QP1:
                    quantise_tokens(parts[1])
                if (s, b) == QW1:
                    quantise_weights(HALF, HALF)
                if b < 3:
                    for tile in slots.get(3 * s + b, []):
                        compress(*tile)
                if b == 1 and s == len(units) - 1:
                    quantise_unit(units[s - 1], whole)
                    quantise_unit(unit, slice(0, PIECE))
        last = units[-1]
        for head in range(2, HEADS):
            quantise_unit(last, slice(head * BLOCK, (head + 1) * BLOCK))
        wr, half, side = groups[-1]
        for first, heads, banks, copies in [
            (0, 2, [TU, TU, KV], [A, A, A]),
            (2, 1, [KV, KV, CH], [A, A, A]),
            (3, 1, [TU, TU, KV], [V, A, V]),
        ]:
            tiles = []
            for m in range(ROW_TILES):
                pool, tag = banks[m]
                open_bank = pool.tile([P, HEADS, BLOCK], F32, name="open_bank", tag=tag)
                compress_pass(open_bank, wr, half, side, first, heads, m, 0)
                tiles.append(open_bank)
            result = out_stage.tile([P, HEADS, ROW_TILES, BLOCK], F32, name="result")
            for m in range(ROW_TILES):
                compress_pass(tiles[m], wr, half, side, first, heads, m, 1)
                copies[m](out=result[:, 0:heads, m, :], in_=tiles[m][:, 0:heads, :])
            nc.sync.dma_start(
                out=outs[half][2 * wr + side, first : first + heads].rearrange("h (n m) d -> n h (m d)", m=ROW_TILES),
                in_=result[:, 0:heads].rearrange("p h m d -> p h (m d)"),
            )
